import numpy as np
import ml_dtypes


def mxq(x, axis, fmt="e4m3"):
    dtype, down = {"e4m3": (ml_dtypes.float8_e4m3fn, 7), "e5m2": (ml_dtypes.float8_e5m2, 14)}[fmt]
    v = np.moveaxis(np.asarray(x, np.float32).astype(ml_dtypes.bfloat16).astype(np.float64), axis, -1)
    blocks = v.reshape(v.shape[:-1] + (-1, 32))
    amax = np.abs(blocks).max(-1, keepdims=True)
    byte = np.maximum(np.where(amax > 0, np.frexp(amax)[1] - 1 + 127, 0) - down, 1)
    scale = np.exp2(byte - 127.0)
    codes = (blocks / scale).astype(np.float32).astype(dtype).astype(np.float64)
    return np.moveaxis((codes * scale).reshape(v.shape), -1, axis)


WIDE = False


def mx_kscale(k):
    if not WIDE:
        return np.ones(k)
    levels = np.array([10, -10, 5, -5, 0])
    if k % 512:
        return np.exp2(np.random.permutation(np.resize(levels, k // 32))).repeat(32)
    a = np.empty((k // 512, 16))
    for p in range(k // 512):
        a[p, :8] = np.random.permutation(np.resize(levels, 8))
        for g in range(8):
            far = levels[np.abs(levels - a[p, g]) >= 10]
            a[p, g + 8] = far[np.random.randint(len(far))]
    return np.exp2(a.ravel()).repeat(32)


BF16 = ml_dtypes.bfloat16


def bf(x):
    return np.asarray(x, np.float32).astype(BF16)


def f64(x):
    return np.asarray(x).astype(np.float64)


B, N, D, E = 2, 2048, 4096, 128

EPS = 1e-6
NUM_ITERS = 8
TEMPERATURE = 1.0
FRAC = 0.7
SEP = 2.0


def logsumexp(t, axis):
    m = t.max(axis=axis, keepdims=True)
    return m + np.log(np.exp(t - m).sum(axis=axis, keepdims=True))


def sinkhorn(t):
    t = np.log(np.maximum(t, EPS))
    t = t / TEMPERATURE
    for _ in range(NUM_ITERS):
        t = t - logsumexp(t, -2)
        t = t - logsumexp(t, -1)
    return np.exp(t)


def draw0():
    s = mx_kscale(D)
    p = np.where(np.random.random(D) < 0.5, 1.0, -1.0)
    side = np.where(np.random.random((B, N, 1)) < FRAC, 1.0, -1.0)
    half = np.where(np.arange(E) < E // 2, 1.0, -1.0)[:, None]
    z = np.random.standard_normal((B, N, D))
    z = z - (z @ p)[..., None] * p / D
    g = np.random.standard_normal((E, D))
    g = g - (g @ p)[:, None] * p / D
    return {"x": bf((z + side * p) * s), "w_gate": bf((g / np.sqrt(D) + SEP * half * p / D) / s)}


def core(x, w_gate):
    gates = mxq(f64(x), 2, "e4m3") @ mxq(f64(w_gate), 1, "e4m3").T
    return sinkhorn(gates)


def e4m3fn_bytes(y):
    return np.clip(np.asarray(y, np.float64), -448.0, 448.0).astype(np.float32).astype(ml_dtypes.float8_e4m3fn).view(np.uint8)


def e4m3fn_values(b):
    return np.asarray(b, np.uint8).view(ml_dtypes.float8_e4m3fn).astype(np.float64)


def setup_inputs():
    d = draw0()
    x0 = np.asarray(d['x']).astype(np.float64)
    s = (np.max(np.abs(x0), axis=(0, 1), keepdims=True) / 448.0).astype(np.float32)
    out = {}
    for k, v in d.items():
        if k == 'x':
            out['x_bytes'] = e4m3fn_bytes(x0 / s.astype(np.float64))
            out['x_scale'] = s
        else:
            out[k] = v
    return out


def reference(x_bytes, x_scale, w_gate):
    return core(e4m3fn_values(x_bytes) * x_scale.astype(np.float64), w_gate)

@@ -1,0 +1,478 @@
+from contextlib import ExitStack
+
+import concourse.mybir as mybir
+from concourse.masks import make_identity
+
+B, N, D, E = 2, 2048, 4096, 128
+EPS = 1e-6
+ROUNDS = 8
+FLOPS = 2 * B * N * D * E
+
+F32 = mybir.dt.float32
+BF16 = mybir.dt.bfloat16
+U32 = mybir.dt.uint32
+U8 = mybir.dt.uint8
+FP8 = mybir.dt.float8_e4m3fn
+FP8X4 = mybir.dt.float8_e4m3fn_x4
+ALU = mybir.AluOpType
+ACT = mybir.ActivationFunctionType
+AX = mybir.AxisListType
+
+P = 128
+TILES = N // P
+NT = B * TILES
+PASSES = D // 512
+AHEAD = 4
+THREE = [(0, 0), (1, 0), (0, 1)]
+SPLIT_GROUPS = [(0, 4), (4, 8), (8, 12), (12, 14), (14, 15), (15, 16)]
+WARM_A = 4
+WARM_B = 0
+WARM_AT = (4, 10)
+FILL_V = 3
+FILL_U = 1
+REP = 12
+HEAD_COLS = 512
+OWN_SKIP = 8
+
+
+def tile_sinkhornrouter_kernel(tc, x_bytes, x_scale, w_gate, out):
+    nc = tc.nc
+    x_view = x_bytes.rearrange("b (p j) k -> b j p k", j=TILES)
+    out_view = out.rearrange("b (p j) e -> b p j e", j=TILES)
+    scale_row = x_scale.rearrange("a b k -> (a b k)")
+
+    with ExitStack() as ctx:
+        const = ctx.enter_context(tc.tile_pool(name="const", bufs=1))
+        byte_pool = ctx.enter_context(tc.tile_pool(name="bytes", bufs=AHEAD))
+        wide_pool = ctx.enter_context(tc.tile_pool(name="wide", bufs=3))
+        grp_pool = ctx.enter_context(tc.tile_pool(name="grp", bufs=4))
+        code_pool = ctx.enter_context(tc.tile_pool(name="code", bufs=3))
+        small = ctx.enter_context(tc.tile_pool(name="small", bufs=4))
+        ps_x = ctx.enter_context(tc.psum_pool(name="psx", bufs=4))
+        ps_1 = ctx.enter_context(tc.psum_pool(name="ps1", bufs=1))
+        ctx.enter_context(tc.manual_schedule())
+
+        ident = const.tile([P, P], F32, name="ident")
+        make_identity(nc, ident[:])
+        ident_bf = const.tile([P, P], BF16, name="ident_bf")
+        make_identity(nc, ident_bf[:])
+        sc = const.tile([P, D], F32, name="sc")
+        sc_own = const.tile([P, 1, 4], F32, name="sc_own")
+        w_raw = const.tile([P, D], BF16, name="w_raw")
+        w_grp = const.tile([P, D], BF16, name="w_grp", align_bytes=64)
+        w_codes = const.tile([P, PASSES * P], U32, name="w_codes", align_bytes=64)
+        w_scl = const.tile([P, PASSES * P], U8, name="w_scl", align_bytes=64)
+        p_t = [const.tile([P, TILES, P], F32, name="p_t%d" % b) for b in range(B)]
+        two_t = [const.tile([P, TILES, 2, P], BF16, name="two_t%d" % b) for b in range(B)]
+        two_b = [const.tile([P, TILES, 2, P], BF16, name="two_b%d" % b) for b in range(B)]
+        p_v = [const.tile([P, TILES, P], F32, name="p_v%d" % b) for b in range(B)]
+        res = [const.tile([P, TILES, P], F32, name="res%d" % b) for b in range(B)]
+        acc = [const.tile([P, TILES], F32, name="acc%d" % b) for b in range(B)]
+        idle = ps_1.tile([P, 512], F32, name="idle")
+
+        byte_tiles = {}
+        wide_tiles = {}
+        grp_tiles = {}
+        held = {}
+
+        def load(i):
+            xb = byte_pool.tile([P, D], U8, name="x_raw_bytes")
+            nc.sync.dma_start(out=xb[:], in_=x_view[i // TILES, i % TILES])
+            byte_tiles[i] = xb
+
+        def own(i):
+            return 0 if i % OWN_SKIP == OWN_SKIP - 1 or i == NT - 1 else 1
+
+        def cast(i):
+            xs = wide_pool.tile([P, D], BF16, name="xs")
+            if own(i) > 0:
+                first = D - 512 * own(i)
+                nc.scalar.copy(out=xs[:, first:], in_=byte_tiles[i][:, first:].bitcast(FP8))
+            wide_tiles[i] = xs
+
+        def widen(i, first, end):
+            cols = slice(first, min(end, D - 512 * own(i)))
+            nc.vector.tensor_tensor(
+                out=wide_tiles[i][:, cols], in0=byte_tiles[i][:, cols].bitcast(FP8), in1=sc[:, cols],
+                op=ALU.mult,
+            )
+
+        def turn(src, grp, own):
+            words = src[:].bitcast(F32)
+            grp_words = grp[:].bitcast(F32)
+            for q in range(PASSES // 2):
+                xt = ps_x.tile([P, 2, 2, P], F32, name="xt")
+                for gg in range(2):
+                    g = 2 * q + gg
+                    for u in range(2):
+                        nc.tensor.transpose(
+                            out=xt[:, gg, u, :],
+                            in_=words[:, 256 * g + u : 256 * (g + 1) : 2],
+                            identity=ident[:],
+                        )
+                plain = min(2, max(0, PASSES - own - 2 * q))
+                if plain > 0:
+                    nc.scalar.copy(
+                        out=grp_words[:, 512 * q : 512 * q + 256 * plain].rearrange(
+                            "p (g r u) -> p g r u", g=plain, u=2
+                        ),
+                        in_=xt[:, 0:plain, :, :].rearrange("p g u r -> p g r u"),
+                    )
+                if plain < 2:
+                    held["xt"] = xt
+
+        def turn_own(grp):
+            g = PASSES - 1
+            for u in range(2):
+                pairs = held["xt"][:, 1, u, :].bitcast(BF16)
+                for e in range(2):
+                    t = 2 * u + e
+                    nc.scalar.activation(
+                        out=grp[:, 512 * g + t : 512 * (g + 1) : 4],
+                        in_=pairs[:, e : 2 * P : 2],
+                        func=ACT.Copy,
+                        scale=sc_own[:, 0, t : t + 1],
+                    )
+
+        def warm(count):
+            for k in range(count):
+                nc.tensor.matmul_mx(
+                    out=idle[:],
+                    lhsT=w_codes[:, 0:P].bitcast(FP8X4),
+                    lhsT_scale=w_scl[:, 0:P],
+                    rhs=w_codes[:, 0:512].bitcast(FP8X4),
+                    rhs_scale=w_scl[:, 0:512],
+                    start=True,
+                    stop=True,
+                )
+
+        def gates(i):
+            b, j = i // TILES, i % TILES
+            codes = code_pool.tile([P, PASSES * P], U32, name="codes", align_bytes=64)
+            scl = code_pool.tile([P, PASSES * P], U8, name="scl", align_bytes=64)
+            nc.vector.quantize_mx(out=codes[:].bitcast(FP8X4), scales=scl[:], in_=grp_tiles[i][:])
+            gps = ps_1.tile([P, P], F32, name="gps")
+            for g in range(PASSES):
+                cols = slice(P * g, P * (g + 1))
+                nc.tensor.matmul_mx(
+                    out=gps[:],
+                    lhsT=w_codes[:, cols].bitcast(FP8X4),
+                    lhsT_scale=w_scl[:, cols],
+                    rhs=codes[:, cols].bitcast(FP8X4),
+                    rhs_scale=scl[:, cols],
+                    start=(g == 0),
+                    stop=(g == PASSES - 1),
+                )
+            nc.scalar.activation(out=p_t[b][:, j, :], in_=gps[:], func=ACT.Relu, bias=-EPS, scale=1.0)
+            nc.scalar.activation(
+                out=two_t[b][:, j, 0, :], in_=p_t[b][:, j, :], func=ACT.Copy, bias=EPS, scale=1.0,
+                accum_out=acc[b][:, j : j + 1],
+            )
+
+        def second_term(b, j0, j1):
+            nc.vector.scalar_tensor_tensor(
+                out=two_t[b][:, j0:j1, 1, :], in0=p_t[b][:, j0:j1, :], scalar=EPS,
+                in1=two_t[b][:, j0:j1, 0, :], op0=ALU.add, op1=ALU.subtract,
+            )
+
+        def flip_terms(b, j0, j1):
+            for a in range(j0, j1, 2):
+                n = min(2, j1 - a)
+                flip = ps_1.tile([P, 2, 2, P], BF16, name="flip")
+                for jj in range(n):
+                    for part in range(2):
+                        nc.tensor.transpose(
+                            out=flip[:, jj, part, :], in_=two_t[b][:, a + jj, part, :],
+                            identity=ident_bf[:],
+                        )
+                nc.scalar.copy(out=two_b[b][:, a : a + n, :, :], in_=flip[:, 0:n, :, :])
+
+        def inverse(den, near, full, pair, lo, hi):
+            if pair is not None:
+                with nc.allow_low_precision(reason="the first of two bfloat16 terms; the second holds what it drops"):
+                    nc.vector.reciprocal(out=pair[:, lo:hi, 0], in_=near)
+            nc.vector.reciprocal(out=full[:, lo:hi], in_=den)
+
+        def rest(full, pair, lo, hi):
+            nc.vector.tensor_tensor(
+                out=pair[:, lo:hi, 1], in0=full[:, lo:hi], in1=pair[:, lo:hi, 0], op=ALU.subtract
+            )
+
+        state = [{}, {}]
+
+        def bank(b, shape):
+            if b == B - 1:
+                return ps_x.tile(shape, F32, name="xt")
+            return ps_1.tile(shape, F32, name="chain")
+
+        def new_v(b, source, summed, near):
+            now = state[b]
+            den = source
+            if not summed:
+                total = small.tile([P, 1], F32, name="total%d" % b)
+                nc.vector.tensor_reduce(out=total[:], in_=source, axis=AX.X, op=ALU.add)
+                den = total[:]
+            v = small.tile([P, 1], F32, name="v%d" % b)
+            vv = small.tile([P, 1, 2], BF16, name="vv%d" % b)
+            inverse(den, den if near is None else near, v, vv, 0, 1)
+            now["v"] = v
+            now["vv"] = vv
+
+        def rest_v(b):
+            rest(state[b]["v"], state[b]["vv"], 0, 1)
+
+        def col_open(b, rep):
+            state[b]["cps"] = bank(b, [P, rep, 2] if rep > 0 else [P, 1])
+
+        def col_sums(b, lo, hi, rep):
+            now = state[b]
+            for j in range(lo, hi):
+                if rep > 0:
+                    for part in range(2):
+                        nc.tensor.matmul(
+                            out=now["cps"][:], lhsT=two_b[b][:, j, part, :],
+                            rhs=now["uu"][:, j : j + 1, :].to_broadcast([P, rep, 2]),
+                            start=(j == 0 and part == 0), stop=(j == TILES - 1 and part == 1),
+                        )
+                    if b == 0 and j in WARM_AT:
+                        warm(1)
+                else:
+                    for n in range(3):
+                        part, term = THREE[n]
+                        nc.tensor.matmul(
+                            out=now["cps"][:], lhsT=two_b[b][:, j, part, :],
+                            rhs=now["uu"][:, j, term : term + 1],
+                            start=(j == 0 and n == 0), stop=(j == TILES - 1 and n == 2),
+                        )
+                    if j in WARM_AT:
+                        warm(1)
+
+        def row_open(b):
+            now = state[b]
+            now["u"] = small.tile([P, TILES], F32, name="u%d" % b)
+            now["uu"] = small.tile([P, TILES, 2], BF16, name="uu%d" % b)
+            now["sums"] = small.tile([P, TILES], F32, name="sums%d" % b)
+
+        def row_sums(b, lo, hi, rep):
+            now = state[b]
+            rps = bank(b, [P, hi - lo, rep, 2] if rep > 0 else [P, hi - lo])
+            for j in range(lo, hi):
+                if rep > 0:
+                    for part in range(2):
+                        nc.tensor.matmul(
+                            out=rps[:, j - lo, :, :], lhsT=two_t[b][:, j, part, :],
+                            rhs=now["vv"][:].to_broadcast([P, rep, 2]),
+                            start=(part == 0), stop=(part == 1),
+                        )
+                    if b == 0 and j in WARM_AT:
+                        warm(1)
+                else:
+                    for n in range(3):
+                        part, term = THREE[n]
+                        nc.tensor.matmul(
+                            out=rps[:, j - lo : j - lo + 1], lhsT=two_t[b][:, j, part, :],
+                            rhs=now["vv"][:, 0, term : term + 1],
+                            start=(n == 0), stop=(n == 2),
+                        )
+                    if j in WARM_AT:
+                        warm(1)
+            now["rps%d" % lo] = rps
+
+        def new_u(b, lo, hi, final, summed):
+            now = state[b]
+            den = now["rps%d" % lo][:]
+            near = den
+            if not summed:
+                nc.vector.tensor_reduce(
+                    out=now["sums"][:, lo:hi], in_=now["rps%d" % lo][:, :, 0, :], axis=AX.X, op=ALU.add
+                )
+                den = now["sums"][:, lo:hi]
+                near = now["rps%d" % lo][:, :, 0, 0]
+            inverse(den, near, now["u"], None if final else now["uu"], lo, hi)
+
+        def rest_u(b, lo, hi):
+            rest(state[b]["u"], state[b]["uu"], lo, hi)
+
+        def scale_columns(b, q, on_vector):
+            v = state[b]["v"]
+            js = slice(4 * q, 4 * q + 4)
+            if on_vector:
+                nc.vector.tensor_scalar(
+                    out=p_v[b][:, js, :], in0=p_t[b][:, js, :], scalar1=EPS, scalar2=v[:, 0:1],
+                    op0=ALU.add, op1=ALU.mult,
+                )
+            else:
+                if "ev" not in state[b]:
+                    ev = small.tile([P, 1], F32, name="ev%d" % b)
+                    nc.scalar.activation(out=ev[:], in_=v[:], func=ACT.Copy, scale=EPS)
+                    state[b]["ev"] = ev
+                nc.scalar.activation(
+                    out=p_v[b][:, js, :], in_=p_t[b][:, js, :], func=ACT.Identity,
+                    scale=v[:, 0:1], bias=state[b]["ev"][:, 0:1],
+                )
+
+        def turn_back(b, q):
+            back = ps_x.tile([P, 4, P], F32, name="xt")
+            for jj in range(4):
+                nc.tensor.transpose(
+                    out=back[:, jj, :], in_=p_v[b][:, 4 * q + jj, :], identity=ident[:]
+                )
+            state[b]["back%d" % q] = back
+
+        def scale_rows(b, q, on_vector):
+            u = state[b]["u"]
+            back = state[b]["back%d" % q]
+            js = slice(4 * q, 4 * q + 4)
+            if on_vector:
+                nc.vector.tensor_tensor(
+                    out=res[b][:, js, :], in0=back[:],
+                    in1=u[:, js].unsqueeze(2).to_broadcast([P, 4, P]), op=ALU.mult,
+                )
+            else:
+                for jj in range(4):
+                    j = 4 * q + jj
+                    nc.scalar.activation(
+                        out=res[b][:, j, :], in_=back[:, jj, :], func=ACT.Copy, scale=u[:, j : j + 1]
+                    )
+            nc.sync.dma_start(out=out_view[b][:, js, :], in_=res[b][:, js, :])
+
+        def early_v_first():
+            new_v(0, acc[0][:], False, None)
+
+        def early_v():
+            new_v(0, state[0]["cps"][:, 0, :], False, state[0]["cps"][:, 0, 0:1])
+
+        def early_u():
+            new_u(0, 0, TILES, False, False)
+
+        def early_rest_v():
+            rest_v(0)
+
+        def early_rest_u():
+            rest_u(0, 0, TILES)
+
+        def early_rows():
+            row_open(0)
+            row_sums(0, 0, TILES, 1)
+
+        def early_cols():
+            col_open(0, 1)
+            col_sums(0, 0, TILES, 1)
+
+        early = [(early_v_first, early_rest_v, early_rows)]
+        for k in range(1, ROUNDS):
+            early.append((early_u, early_rest_u, early_cols))
+            early.append((early_v, early_rest_v, early_rows))
+
+        load(0)
+        for c in range(4):
+            cols = slice(1024 * c, 1024 * (c + 1))
+            nc.sync.dma_start(out=sc[:, cols], in_=scale_row[cols].partition_broadcast(P))
+        nc.sync.dma_start(
+            out=sc_own[:],
+            in_=x_scale.rearrange("a b (g p t) -> p (a b g) t", p=P, t=4)[:, PASSES - 1 :, :],
+        )
+        load(1)
+        cast(0)
+        nc.sync.dma_start(out=w_raw[:], in_=w_gate)
+        for i in range(2, AHEAD):
+            load(i)
+
+        EARLY_FROM = TILES + 2
+        LAST_EARLY = NT
+        done = 0
+        pending = []
+        for i in range(NT + 2):
+            if i == 0:
+                for c in range(4):
+                    widen(i, 1024 * c, 1024 * (c + 1))
+            elif i < NT and len(pending) > 0:
+                widen(i, 0, HEAD_COLS)
+            elif i < NT:
+                widen(i, 0, D)
+            for entry in pending:
+                entry[1]()
+                entry[2]()
+                warm(WARM_B)
+            if 0 < i < NT and len(pending) > 0:
+                widen(i, HEAD_COLS, D)
+            pending.clear()
+            if i < NT:
+                if i + AHEAD < NT:
+                    load(i + AHEAD)
+                grp_tiles[i] = grp_pool.tile([P, D], BF16, name="grp", align_bytes=64)
+                turn(wide_tiles[i], grp_tiles[i], own(i))
+            if i < 2 and own(i) > 0:
+                turn_own(grp_tiles[i])
+            if i == 0:
+                turn(w_raw, w_grp, 0)
+            if i == 2:
+                nc.vector.quantize_mx(out=w_codes[:].bitcast(FP8X4), scales=w_scl[:], in_=w_grp[:])
+            k = i - 3
+            if k >= 0:
+                for j0, j1 in SPLIT_GROUPS:
+                    if k % TILES == j1 - 1:
+                        second_term(k // TILES, j0, j1)
+                        flip_terms(k // TILES, j0, j1)
+            if i >= 2:
+                gates(i - 2)
+            if 2 <= i < NT and own(i) > 0:
+                turn_own(grp_tiles[i])
+            if i + 1 < NT:
+                cast(i + 1)
+            if EARLY_FROM <= i < LAST_EARLY and done < len(early):
+                early[done][0]()
+                pending.append(early[done])
+                done += 1
+            elif 2 <= i < NT:
+                warm(WARM_A)
+
+        last = B - 1
+        halves = [(0, TILES // 2), (TILES // 2, TILES)]
+        left = early[done:]
+        left[0][0]()
+        left[0][1]()
+        left[0][2]()
+        assert len(left) == 1
+        for q in range(4):
+            scale_columns(0, q, False)
+        new_v(last, acc[last][:], False, None)
+        rest_v(last)
+        second_term(last, TILES - 1, TILES)
+        for rnd in range(ROUNDS):
+            final = rnd == ROUNDS - 1
+            row_open(last)
+            for lo, hi in halves:
+                row_sums(last, lo, hi, REP)
+            if rnd == 0:
+                flip_terms(last, TILES - 1, TILES)
+                new_u(0, 0, TILES, True, False)
+            if final:
+                scale_columns(last, 0, True)
+                scale_columns(last, 1, True)
+                scale_columns(last, 2, False)
+                scale_columns(last, 3, False)
+                for lo, hi in halves:
+                    new_u(last, lo, hi, True, False)
+                for q in range(4):
+                    turn_back(last, q)
+                    scale_rows(last, q, q % 2 == 0)
+            else:
+                if rnd < 2:
+                    turn_back(0, 2 * rnd)
+                    scale_rows(0, 2 * rnd, False)
+                else:
+                    warm(FILL_U)
+                col_open(last, REP)
+                for lo, hi in halves:
+                    new_u(last, lo, hi, False, False)
+                    rest_u(last, lo, hi)
+                    col_sums(last, lo, hi, REP)
+                if rnd < 2:
+                    turn_back(0, 2 * rnd + 1)
+                    scale_rows(0, 2 * rnd + 1, False)
+                    warm(FILL_V - 2)
+                else:
+                    warm(FILL_V)
+                new_v(last, state[last]["cps"][:, 0, :], False, state[last]["cps"][:, 0, 0:1])
+                rest_v(last)

@@ -28,9 +28,11 @@ SPLIT_GROUPS = [(0, 4), (4, 8), (8, 12), (12, 14), (14, 15), (15, 16)]
 WARM_A = 4
 WARM_B = 0
 WARM_AT = (4, 10)
-FILL_V = 3
+FILL_V = 2
 FILL_U = 1
 REP = 12
+W_LO = 24
+W_ALL = W_LO + 2 * REP
 HEAD_COLS = 512
 OWN_SKIP = 8
 
@@ -429,6 +431,7 @@ def tile_sinkhornrouter_kernel(tc, x_bytes, x_scale, w_gate, out):
 
         last = B - 1
         halves = [(0, TILES // 2), (TILES // 2, TILES)]
+        now = state[last]
         left = early[done:]
         left[0][0]()
         left[0][1]()
@@ -436,14 +439,108 @@ def tile_sinkhornrouter_kernel(tc, x_bytes, x_scale, w_gate, out):
         assert len(left) == 1
         for q in range(4):
             scale_columns(0, q, False)
-        new_v(last, acc[last][:], False, None)
-        rest_v(last)
-        second_term(last, TILES - 1, TILES)
+
+        def low_precision():
+            return nc.allow_low_precision(reason="the first of two bfloat16 terms; the second holds what it drops")
+
+        def v_open():
+            now["v"] = small.tile([P, 1], F32, name="v%d" % last)
+            now["vv"] = small.tile([P, 2, 1], BF16, name="vv%d" % last)
+            now["total"] = small.tile([P, 1], F32, name="total%d" % last)
+
+        def v_first(near):
+            with low_precision():
+                nc.vector.reciprocal(out=now["vv"][:, 0, :], in_=near)
+
+        def v_sum(source):
+            nc.vector.tensor_reduce(out=now["total"][:], in_=source, axis=AX.X, op=ALU.add)
+
+        def v_full():
+            nc.vector.reciprocal(out=now["v"][:], in_=now["total"][:])
+
+        def v_second():
+            nc.vector.tensor_tensor(
+                out=now["vv"][:, 1, :], in0=now["v"][:], in1=now["vv"][:, 0, :], op=ALU.subtract
+            )
+
+        def rows_open():
+            now["u"] = small.tile([P, TILES], F32, name="u%d" % last)
+            now["uu"] = small.tile([P, 2, TILES], BF16, name="uu%d" % last)
+            now["sums"] = small.tile([P, TILES], F32, name="sums%d" % last)
+            for lo, hi in halves:
+                now["rps%d" % lo] = ps_x.tile([P, hi - lo, W_ALL], F32, name="xt")
+
+        def rows(part, j0, j1):
+            for j in range(j0, j1):
+                lo = [a for a, b in halves if a <= j < b][0]
+                rps = now["rps%d" % lo]
+                if part == 1:
+                    nc.tensor.matmul(
+                        out=rps[:, j - lo, 0:W_LO], lhsT=two_t[last][:, j, 1, :],
+                        rhs=now["vv"][:, 0, :].to_broadcast([P, W_LO]), start=True, stop=True,
+                    )
+                else:
+                    nc.tensor.matmul(
+                        out=rps[:, j - lo, W_LO:W_ALL].rearrange("p (r t) -> p r t", t=2),
+                        lhsT=two_t[last][:, j, 0, :],
+                        rhs=now["vv"][:].rearrange("p t o -> p o t").to_broadcast([P, REP, 2]),
+                        start=True, stop=True,
+                    )
+
+        def u_first(lo, hi):
+            with low_precision():
+                nc.vector.reciprocal(out=now["uu"][:, 0, lo:hi], in_=now["rps%d" % lo][:, :, W_LO])
+
+        def u_sum(lo, hi):
+            nc.vector.tensor_reduce(
+                out=now["sums"][:, lo:hi], in_=now["rps%d" % lo][:, :, W_LO - 1 : W_LO + 2], axis=AX.X, op=ALU.add
+            )
+
+        def u_full(lo, hi):
+            nc.vector.reciprocal(out=now["u"][:, lo:hi], in_=now["sums"][:, lo:hi])
+
+        def u_second(lo, hi):
+            nc.vector.tensor_tensor(
+                out=now["uu"][:, 1, lo:hi], in0=now["u"][:, lo:hi], in1=now["uu"][:, 0, lo:hi], op=ALU.subtract
+            )
+
+        def cols(part, j0, j1):
+            cps = now["cps"]
+            for j in range(j0, j1):
+                if part == 1:
+                    nc.tensor.matmul(
+                        out=cps[:, 0:W_LO], lhsT=two_b[last][:, j, 1, :],
+                        rhs=now["uu"][:, 0, j : j + 1].to_broadcast([P, W_LO]),
+                        start=(j == 0), stop=(j == TILES - 1),
+                    )
+                else:
+                    nc.tensor.matmul(
+                        out=cps[:, W_LO:W_ALL].rearrange("p (r t) -> p r t", t=2),
+                        lhsT=two_b[last][:, j, 0, :],
+                        rhs=now["uu"][:, :, j : j + 1].rearrange("p t o -> p o t").to_broadcast([P, REP, 2]),
+                        start=(j == 0), stop=(j == TILES - 1),
+                    )
+
+        (a0, a1), (b0, b1) = halves
+        v_open()
+        v_sum(acc[last][:])
+        v_first(now["total"][:])
         for rnd in range(ROUNDS):
             final = rnd == ROUNDS - 1
-            row_open(last)
-            for lo, hi in halves:
-                row_sums(last, lo, hi, REP)
+            rows_open()
+            if rnd == 0:
+                rows(1, 0, TILES - 1)
+                second_term(last, TILES - 1, TILES)
+                v_full()
+                v_second()
+                rows(1, TILES - 1, TILES)
+            else:
+                rows(1, 0, TILES)
+                v_sum(now["cps"][:, W_LO - 1 : W_LO + 2])
+                v_full()
+                v_second()
+            rows(0, a0, a1)
+            rows(0, b0, b1)
             if rnd == 0:
                 flip_terms(last, TILES - 1, TILES)
                 new_u(0, 0, TILES, True, False)
@@ -453,7 +550,8 @@ def tile_sinkhornrouter_kernel(tc, x_bytes, x_scale, w_gate, out):
                 scale_columns(last, 2, False)
                 scale_columns(last, 3, False)
                 for lo, hi in halves:
-                    new_u(last, lo, hi, True, False)
+                    u_sum(lo, hi)
+                    u_full(lo, hi)
                 for q in range(4):
                     turn_back(last, q)
                     scale_rows(last, q, q % 2 == 0)
@@ -463,16 +561,24 @@ def tile_sinkhornrouter_kernel(tc, x_bytes, x_scale, w_gate, out):
                     scale_rows(0, 2 * rnd, False)
                 else:
                     warm(FILL_U)
-                col_open(last, REP)
-                for lo, hi in halves:
-                    new_u(last, lo, hi, False, False)
-                    rest_u(last, lo, hi)
-                    col_sums(last, lo, hi, REP)
+                now["cps"] = ps_x.tile([P, W_ALL], F32, name="xt")
+                u_first(a0, a1)
+                u_sum(a0, a1)
+                u_first(b0, b1)
+                cols(1, a0, a1)
+                u_full(a0, a1)
+                u_sum(b0, b1)
+                cols(1, b0, b1)
+                u_second(a0, a1)
+                u_full(b0, b1)
+                cols(0, a0, a1)
+                u_second(b0, b1)
+                cols(0, b0, b1)
                 if rnd < 2:
                     turn_back(0, 2 * rnd + 1)
                     scale_rows(0, 2 * rnd + 1, False)
-                    warm(FILL_V - 2)
+                    warm(max(0, FILL_V - 2))
                 else:
                     warm(FILL_V)
-                new_v(last, state[last]["cps"][:, 0, :], False, state[last]["cps"][:, 0, 0:1])
-                rest_v(last)
+                v_open()
+                v_first(now["cps"][:, W_LO : W_LO + 1])

@@ -69,7 +69,9 @@ def tile_sinkhornrouter_kernel(tc, x_bytes, x_scale, w_gate, out):
         two_b = [const.tile([P, TILES, 2, P], BF16, name="two_b%d" % b) for b in range(B)]
         p_v = [const.tile([P, TILES, P], F32, name="p_v%d" % b) for b in range(B)]
         res = [const.tile([P, TILES, P], F32, name="res%d" % b) for b in range(B)]
-        acc = [const.tile([P, TILES], F32, name="acc%d" % b) for b in range(B)]
+        acc = [const.tile([P, TILES + 1], F32, name="acc%d" % b) for b in range(B)]
+        for b in range(B):
+            nc.gpsimd.memset(acc[b][:, TILES : TILES + 1], N * EPS)
         idle = ps_1.tile([P, 512], F32, name="idle")
 
         byte_tiles = {}
@@ -153,7 +155,10 @@ def tile_sinkhornrouter_kernel(tc, x_bytes, x_scale, w_gate, out):
             codes = code_pool.tile([P, PASSES * P], U32, name="codes", align_bytes=64)
             scl = code_pool.tile([P, PASSES * P], U8, name="scl", align_bytes=64)
             nc.vector.quantize_mx(out=codes[:].bitcast(FP8X4), scales=scl[:], in_=grp_tiles[i][:])
-            gps = ps_1.tile([P, P], F32, name="gps")
+            if i >= NT - 2:
+                gps = ps_x.tile([P, P], F32, name="xt")
+            else:
+                gps = ps_1.tile([P, P], F32, name="gps")
             for g in range(PASSES):
                 cols = slice(P * g, P * (g + 1))
                 nc.tensor.matmul_mx(
@@ -165,11 +170,11 @@ def tile_sinkhornrouter_kernel(tc, x_bytes, x_scale, w_gate, out):
                     start=(g == 0),
                     stop=(g == PASSES - 1),
                 )
-            nc.scalar.activation(out=p_t[b][:, j, :], in_=gps[:], func=ACT.Relu, bias=-EPS, scale=1.0)
             nc.scalar.activation(
-                out=two_t[b][:, j, 0, :], in_=p_t[b][:, j, :], func=ACT.Copy, bias=EPS, scale=1.0,
+                out=p_t[b][:, j, :], in_=gps[:], func=ACT.Relu, bias=-EPS, scale=1.0,
                 accum_out=acc[b][:, j : j + 1],
             )
+            nc.scalar.activation(out=two_t[b][:, j, 0, :], in_=p_t[b][:, j, :], func=ACT.Copy, bias=EPS, scale=1.0)
 
         def second_term(b, j0, j1):
             nc.vector.scalar_tensor_tensor(
@@ -177,10 +182,13 @@ def tile_sinkhornrouter_kernel(tc, x_bytes, x_scale, w_gate, out):
                 in1=two_t[b][:, j0:j1, 0, :], op0=ALU.add, op1=ALU.subtract,
             )
 
-        def flip_terms(b, j0, j1):
+        def flip_terms(b, j0, j1, spare=False):
             for a in range(j0, j1, 2):
                 n = min(2, j1 - a)
-                flip = ps_1.tile([P, 2, 2, P], BF16, name="flip")
+                if spare:
+                    flip = ps_x.tile([P, 2, 2, P], BF16, name="xt")
+                else:
+                    flip = ps_1.tile([P, 2, 2, P], BF16, name="flip")
                 for jj in range(n):
                     for part in range(2):
                         nc.tensor.transpose(
@@ -236,7 +244,7 @@ def tile_sinkhornrouter_kernel(tc, x_bytes, x_scale, w_gate, out):
                             rhs=now["uu"][:, j : j + 1, :].to_broadcast([P, rep, 2]),
                             start=(j == 0 and part == 0), stop=(j == TILES - 1 and part == 1),
                         )
-                    if b == 0 and j in WARM_AT:
+                    if b == 0 and j in WARM_AT and len(quiet) == 0:
                         warm(1)
                 else:
                     for n in range(3):
@@ -266,7 +274,7 @@ def tile_sinkhornrouter_kernel(tc, x_bytes, x_scale, w_gate, out):
                             rhs=now["vv"][:].to_broadcast([P, rep, 2]),
                             start=(part == 0), stop=(part == 1),
                         )
-                    if b == 0 and j in WARM_AT:
+                    if b == 0 and j in WARM_AT and len(quiet) == 0:
                         warm(1)
                 else:
                     for n in range(3):
@@ -384,6 +392,8 @@ def tile_sinkhornrouter_kernel(tc, x_bytes, x_scale, w_gate, out):
         LAST_EARLY = NT
         done = 0
         pending = []
+        quiet = []
+        late = []
         for i in range(NT + 2):
             if i == 0:
                 for c in range(4):
@@ -396,7 +406,10 @@ def tile_sinkhornrouter_kernel(tc, x_bytes, x_scale, w_gate, out):
                 entry[1]()
                 entry[2]()
                 warm(WARM_B)
-            if 0 < i < NT and len(pending) > 0:
+            if i == NT - 1:
+                for first in (HEAD_COLS, 1024, 2048, 3072):
+                    widen(i, first, max(1024, first + 1024 - first % 1024))
+            elif 0 < i < NT and len(pending) > 0:
                 widen(i, HEAD_COLS, D)
             pending.clear()
             if i < NT:
@@ -413,9 +426,11 @@ def tile_sinkhornrouter_kernel(tc, x_bytes, x_scale, w_gate, out):
             k = i - 3
             if k >= 0:
                 for j0, j1 in SPLIT_GROUPS:
-                    if k % TILES == j1 - 1:
+                    if k % TILES == j1 - 1 and i < NT:
                         second_term(k // TILES, j0, j1)
                         flip_terms(k // TILES, j0, j1)
+                    elif k % TILES == j1 - 1:
+                        late.append((k // TILES, j0, j1))
             if i >= 2:
                 gates(i - 2)
             if 2 <= i < NT and own(i) > 0:
@@ -435,10 +450,12 @@ def tile_sinkhornrouter_kernel(tc, x_bytes, x_scale, w_gate, out):
         left = early[done:]
         left[0][0]()
         left[0][1]()
+        quiet.append(1)
         left[0][2]()
         assert len(left) == 1
-        for q in range(4):
-            scale_columns(0, q, False)
+        for entry in late:
+            second_term(entry[0], entry[1], entry[2])
+            flip_terms(entry[0], entry[1], entry[2], entry[1] == TILES - 2)
 
         def low_precision():
             return nc.allow_low_precision(reason="the first of two bfloat16 terms; the second holds what it drops")
@@ -543,7 +560,8 @@ def tile_sinkhornrouter_kernel(tc, x_bytes, x_scale, w_gate, out):
             rows(0, b0, b1)
             if rnd == 0:
                 flip_terms(last, TILES - 1, TILES)
-                new_u(0, 0, TILES, True, False)
+                for q in range(4):
+                    scale_columns(0, q, False)
             if final:
                 scale_columns(last, 0, True)
                 scale_columns(last, 1, True)
@@ -556,10 +574,10 @@ def tile_sinkhornrouter_kernel(tc, x_bytes, x_scale, w_gate, out):
                     turn_back(last, q)
                     scale_rows(last, q, q % 2 == 0)
             else:
-                if rnd < 2:
-                    turn_back(0, 2 * rnd)
-                    scale_rows(0, 2 * rnd, False)
-                else:
+                if 1 <= rnd <= 2:
+                    turn_back(0, 2 * rnd - 1)
+                    scale_rows(0, 2 * rnd - 1, False)
+                elif rnd > 2:
                     warm(FILL_U)
                 now["cps"] = ps_x.tile([P, W_ALL], F32, name="xt")
                 u_first(a0, a1)
@@ -574,9 +592,11 @@ def tile_sinkhornrouter_kernel(tc, x_bytes, x_scale, w_gate, out):
                 cols(0, a0, a1)
                 u_second(b0, b1)
                 cols(0, b0, b1)
+                if rnd == 0:
+                    new_u(0, 0, TILES, True, False)
                 if rnd < 2:
-                    turn_back(0, 2 * rnd + 1)
-                    scale_rows(0, 2 * rnd + 1, False)
+                    turn_back(0, 2 * rnd)
+                    scale_rows(0, 2 * rnd, False)
                     warm(max(0, FILL_V - 2))
                 else:
                     warm(FILL_V)

@@ -27,7 +27,8 @@ THREE = [(0, 0), (1, 0), (0, 1)]
 SPLIT_GROUPS = [(0, 4), (4, 8), (8, 12), (12, 14), (14, 15), (15, 16)]
 WARM_A = 4
 WARM_B = 0
-WARM_AT = (4, 10)
+WARM_C = 2
+WARM_AT = ()
 FILL_V = 2
 FILL_U = 1
 REP = 12
@@ -406,6 +407,10 @@ def tile_sinkhornrouter_kernel(tc, x_bytes, x_scale, w_gate, out):
                 entry[1]()
                 entry[2]()
                 warm(WARM_B)
+            ahead = 0 < i < NT - 1 and len(pending) > 0
+            if ahead:
+                gates(i - 2)
+                warm(WARM_C)
             if i == NT - 1:
                 for first in (HEAD_COLS, 1024, 2048, 3072):
                     widen(i, first, max(1024, first + 1024 - first % 1024))
@@ -431,7 +436,7 @@ def tile_sinkhornrouter_kernel(tc, x_bytes, x_scale, w_gate, out):
                         flip_terms(k // TILES, j0, j1)
                     elif k % TILES == j1 - 1:
                         late.append((k // TILES, j0, j1))
-            if i >= 2:
+            if i >= 2 and not ahead:
                 gates(i - 2)
             if 2 <= i < NT and own(i) > 0:
                 turn_own(grp_tiles[i])
@@ -553,7 +558,6 @@ def tile_sinkhornrouter_kernel(tc, x_bytes, x_scale, w_gate, out):
                 rows(1, TILES - 1, TILES)
             else:
                 rows(1, 0, TILES)
-                v_sum(now["cps"][:, W_LO - 1 : W_LO + 2])
                 v_full()
                 v_second()
             rows(0, a0, a1)
@@ -580,15 +584,15 @@ def tile_sinkhornrouter_kernel(tc, x_bytes, x_scale, w_gate, out):
                 elif rnd > 2:
                     warm(FILL_U)
                 now["cps"] = ps_x.tile([P, W_ALL], F32, name="xt")
-                u_first(a0, a1)
                 u_sum(a0, a1)
-                u_first(b0, b1)
+                u_first(a0, a1)
                 cols(1, a0, a1)
-                u_full(a0, a1)
                 u_sum(b0, b1)
+                u_full(a0, a1)
+                u_first(b0, b1)
                 cols(1, b0, b1)
-                u_second(a0, a1)
                 u_full(b0, b1)
+                u_second(a0, a1)
                 cols(0, a0, a1)
                 u_second(b0, b1)
                 cols(0, b0, b1)
@@ -601,4 +605,5 @@ def tile_sinkhornrouter_kernel(tc, x_bytes, x_scale, w_gate, out):
                 else:
                     warm(FILL_V)
                 v_open()
+                v_sum(now["cps"][:, W_LO - 1 : W_LO + 2])
                 v_first(now["cps"][:, W_LO : W_LO + 1])

@@ -23,6 +23,7 @@ TILES = N // P
 NT = B * TILES
 PASSES = D // 512
 AHEAD = 4
+FIRST = 2
 THREE = [(0, 0), (1, 0), (0, 1)]
 SPLIT_GROUPS = [(0, 4), (4, 8), (8, 12), (12, 14), (14, 15), (15, 16)]
 WARM_A = 4
@@ -86,7 +87,7 @@ def tile_sinkhornrouter_kernel(tc, x_bytes, x_scale, w_gate, out):
             byte_tiles[i] = xb
 
         def own(i):
-            return 0 if i % OWN_SKIP == OWN_SKIP - 1 or i == NT - 1 else 1
+            return 0 if i % OWN_SKIP == OWN_SKIP - 1 or i == NT - 1 or i < FIRST else 1
 
         def cast(i):
             xs = wide_pool.tile([P, D], BF16, name="xs")
@@ -102,10 +103,10 @@ def tile_sinkhornrouter_kernel(tc, x_bytes, x_scale, w_gate, out):
                 op=ALU.mult,
             )
 
-        def turn(src, grp, own):
+        def turn(src, grp, own, q0=0, q1=PASSES // 2):
             words = src[:].bitcast(F32)
             grp_words = grp[:].bitcast(F32)
-            for q in range(PASSES // 2):
+            for q in range(q0, q1):
                 xt = ps_x.tile([P, 2, 2, P], F32, name="xt")
                 for gg in range(2):
                     g = 2 * q + gg
@@ -375,19 +376,27 @@ def tile_sinkhornrouter_kernel(tc, x_bytes, x_scale, w_gate, out):
             early.append((early_u, early_rest_u, early_cols))
             early.append((early_v, early_rest_v, early_rows))
 
-        load(0)
+        for i in range(FIRST):
+            byte_tiles[i] = byte_pool.tile([P, D], U8, name="x_raw_bytes")
+            wide_tiles[i] = wide_pool.tile([P, D], BF16, name="xs")
+            grp_tiles[i] = grp_pool.tile([P, D], BF16, name="grp", align_bytes=64)
         for c in range(4):
             cols = slice(1024 * c, 1024 * (c + 1))
             nc.sync.dma_start(out=sc[:, cols], in_=scale_row[cols].partition_broadcast(P))
+            for i in range(FIRST):
+                nc.sync.dma_start(out=byte_tiles[i][:, cols], in_=x_view[0, i][:, cols])
         nc.sync.dma_start(
             out=sc_own[:],
             in_=x_scale.rearrange("a b (g p t) -> p (a b g) t", p=P, t=4)[:, PASSES - 1 :, :],
         )
-        load(1)
-        cast(0)
+        load(FIRST)
         nc.sync.dma_start(out=w_raw[:], in_=w_gate)
-        for i in range(2, AHEAD):
+        for i in range(FIRST + 1, AHEAD):
             load(i)
+        for c in range(4):
+            for i in range(FIRST):
+                widen(i, 1024 * c, 1024 * (c + 1))
+                turn(wide_tiles[i], grp_tiles[i], 0, c, c + 1)
 
         EARLY_FROM = TILES + 2
         LAST_EARLY = NT
@@ -396,9 +405,8 @@ def tile_sinkhornrouter_kernel(tc, x_bytes, x_scale, w_gate, out):
         quiet = []
         late = []
         for i in range(NT + 2):
-            if i == 0:
-                for c in range(4):
-                    widen(i, 1024 * c, 1024 * (c + 1))
+            if i < FIRST:
+                at = 0
             elif i < NT and len(pending) > 0:
                 widen(i, 0, HEAD_COLS)
             elif i < NT:
@@ -420,10 +428,9 @@ def tile_sinkhornrouter_kernel(tc, x_bytes, x_scale, w_gate, out):
             if i < NT:
                 if i + AHEAD < NT:
                     load(i + AHEAD)
+            if FIRST <= i < NT:
                 grp_tiles[i] = grp_pool.tile([P, D], BF16, name="grp", align_bytes=64)
                 turn(wide_tiles[i], grp_tiles[i], own(i))
-            if i < 2 and own(i) > 0:
-                turn_own(grp_tiles[i])
             if i == 0:
                 turn(w_raw, w_grp, 0)
             if i == 2:
@@ -440,7 +447,7 @@ def tile_sinkhornrouter_kernel(tc, x_bytes, x_scale, w_gate, out):
                 gates(i - 2)
             if 2 <= i < NT and own(i) > 0:
                 turn_own(grp_tiles[i])
-            if i + 1 < NT:
+            if FIRST <= i + 1 < NT:
                 cast(i + 1)
             if EARLY_FROM <= i < LAST_EARLY and done < len(early):
                 early[done][0]()

@@ -35,7 +35,7 @@ FILL_U = 1
 REP = 12
 W_LO = 24
 W_ALL = W_LO + 2 * REP
-HEAD_COLS = 512
+HEAD_COLS = 1024
 OWN_SKIP = 8
 
 
@@ -87,7 +87,7 @@ def tile_sinkhornrouter_kernel(tc, x_bytes, x_scale, w_gate, out):
             byte_tiles[i] = xb
 
         def own(i):
-            return 0 if i % OWN_SKIP == OWN_SKIP - 1 or i == NT - 1 or i < FIRST else 1
+            return 0 if i == NT - 1 or i < FIRST else 1
 
         def cast(i):
             xs = wide_pool.tile([P, D], BF16, name="xs")
@@ -420,8 +420,8 @@ def tile_sinkhornrouter_kernel(tc, x_bytes, x_scale, w_gate, out):
                 gates(i - 2)
                 warm(WARM_C)
             if i == NT - 1:
-                for first in (HEAD_COLS, 1024, 2048, 3072):
-                    widen(i, first, max(1024, first + 1024 - first % 1024))
+                for first in range(HEAD_COLS, D, 1024):
+                    widen(i, first, first + 1024)
             elif 0 < i < NT and len(pending) > 0:
                 widen(i, HEAD_COLS, D)
             pending.clear()

@@ -36,6 +36,7 @@ REP = 12
 W_LO = 24
 W_ALL = W_LO + 2 * REP
 HEAD_COLS = 1024
+OWN_TWO = (21, 25)
 OWN_SKIP = 8
 
 
@@ -61,7 +62,7 @@ def tile_sinkhornrouter_kernel(tc, x_bytes, x_scale, w_gate, out):
         ident_bf = const.tile([P, P], BF16, name="ident_bf")
         make_identity(nc, ident_bf[:])
         sc = const.tile([P, D], F32, name="sc")
-        sc_own = const.tile([P, 1, 4], F32, name="sc_own")
+        sc_own = const.tile([P, 2, 4], F32, name="sc_own")
         w_raw = const.tile([P, D], BF16, name="w_raw")
         w_grp = const.tile([P, D], BF16, name="w_grp", align_bytes=64)
         w_codes = const.tile([P, PASSES * P], U32, name="w_codes", align_bytes=64)
@@ -87,7 +88,9 @@ def tile_sinkhornrouter_kernel(tc, x_bytes, x_scale, w_gate, out):
             byte_tiles[i] = xb
 
         def own(i):
-            return 0 if i == NT - 1 or i < FIRST else 1
+            if i == NT - 1 or i < FIRST:
+                return 0
+            return 2 if i in OWN_TWO else 1
 
         def cast(i):
             xs = wide_pool.tile([P, D], BF16, name="xs")
@@ -127,18 +130,19 @@ def tile_sinkhornrouter_kernel(tc, x_bytes, x_scale, w_gate, out):
                 if plain < 2:
                     held["xt"] = xt
 
-        def turn_own(grp):
-            g = PASSES - 1
-            for u in range(2):
-                pairs = held["xt"][:, 1, u, :].bitcast(BF16)
-                for e in range(2):
-                    t = 2 * u + e
-                    nc.scalar.activation(
-                        out=grp[:, 512 * g + t : 512 * (g + 1) : 4],
-                        in_=pairs[:, e : 2 * P : 2],
-                        func=ACT.Copy,
-                        scale=sc_own[:, 0, t : t + 1],
-                    )
+        def turn_own(grp, count):
+            for gg in range(2 - count, 2):
+                g = PASSES - 2 + gg
+                for u in range(2):
+                    pairs = held["xt"][:, gg, u, :].bitcast(BF16)
+                    for e in range(2):
+                        t = 2 * u + e
+                        nc.scalar.activation(
+                            out=grp[:, 512 * g + t : 512 * (g + 1) : 4],
+                            in_=pairs[:, e : 2 * P : 2],
+                            func=ACT.Copy,
+                            scale=sc_own[:, gg, t : t + 1],
+                        )
 
         def warm(count):
             for k in range(count):
@@ -387,7 +391,7 @@ def tile_sinkhornrouter_kernel(tc, x_bytes, x_scale, w_gate, out):
                 nc.sync.dma_start(out=byte_tiles[i][:, cols], in_=x_view[0, i][:, cols])
         nc.sync.dma_start(
             out=sc_own[:],
-            in_=x_scale.rearrange("a b (g p t) -> p (a b g) t", p=P, t=4)[:, PASSES - 1 :, :],
+            in_=x_scale.rearrange("a b (g p t) -> p (a b g) t", p=P, t=4)[:, PASSES - 2 :, :],
         )
         load(FIRST)
         nc.sync.dma_start(out=w_raw[:], in_=w_gate)
@@ -446,7 +450,7 @@ def tile_sinkhornrouter_kernel(tc, x_bytes, x_scale, w_gate, out):
             if i >= 2 and not ahead:
                 gates(i - 2)
             if 2 <= i < NT and own(i) > 0:
-                turn_own(grp_tiles[i])
+                turn_own(grp_tiles[i], own(i))
             if FIRST <= i + 1 < NT:
                 cast(i + 1)
             if EARLY_FROM <= i < LAST_EARLY and done < len(early):

@@ -28,7 +28,7 @@ THREE = [(0, 0), (1, 0), (0, 1)]
 SPLIT_GROUPS = [(0, 4), (4, 8), (8, 12), (12, 14), (14, 15), (15, 16)]
 WARM_A = 4
 WARM_B = 0
-WARM_C = 2
+WARM_C = 0
 WARM_AT = ()
 FILL_V = 2
 FILL_U = 1

@@ -32,11 +32,12 @@ WARM_C = 0
 WARM_AT = ()
 FILL_V = 2
 FILL_U = 1
-REP = 12
-W_LO = 24
-W_ALL = W_LO + 2 * REP
+WIDE_ROUNDS = 3
+WIDE = 32
+NARROW = 12
 HEAD_COLS = 1024
 OWN_TWO = (21, 25)
+LAST_PIECES = [(0, 4), (4, 6), (6, 8)]
 OWN_SKIP = 8
 
 
@@ -160,22 +161,26 @@ def tile_sinkhornrouter_kernel(tc, x_bytes, x_scale, w_gate, out):
             b, j = i // TILES, i % TILES
             codes = code_pool.tile([P, PASSES * P], U32, name="codes", align_bytes=64)
             scl = code_pool.tile([P, PASSES * P], U8, name="scl", align_bytes=64)
-            nc.vector.quantize_mx(out=codes[:].bitcast(FP8X4), scales=scl[:], in_=grp_tiles[i][:])
             if i >= NT - 2:
                 gps = ps_x.tile([P, P], F32, name="xt")
             else:
                 gps = ps_1.tile([P, P], F32, name="gps")
-            for g in range(PASSES):
-                cols = slice(P * g, P * (g + 1))
-                nc.tensor.matmul_mx(
-                    out=gps[:],
-                    lhsT=w_codes[:, cols].bitcast(FP8X4),
-                    lhsT_scale=w_scl[:, cols],
-                    rhs=codes[:, cols].bitcast(FP8X4),
-                    rhs_scale=scl[:, cols],
-                    start=(g == 0),
-                    stop=(g == PASSES - 1),
+            for g0, g1 in LAST_PIECES if i == NT - 1 else [(0, PASSES)]:
+                part = slice(P * g0, P * g1)
+                nc.vector.quantize_mx(
+                    out=codes[:, part].bitcast(FP8X4), scales=scl[:, part], in_=grp_tiles[i][:, 512 * g0 : 512 * g1]
                 )
+                for g in range(g0, g1):
+                    cols = slice(P * g, P * (g + 1))
+                    nc.tensor.matmul_mx(
+                        out=gps[:],
+                        lhsT=w_codes[:, cols].bitcast(FP8X4),
+                        lhsT_scale=w_scl[:, cols],
+                        rhs=codes[:, cols].bitcast(FP8X4),
+                        rhs_scale=scl[:, cols],
+                        start=(g == 0),
+                        stop=(g == PASSES - 1),
+                    )
             nc.scalar.activation(
                 out=p_t[b][:, j, :], in_=gps[:], func=ACT.Relu, bias=-EPS, scale=1.0,
                 accum_out=acc[b][:, j : j + 1],
@@ -496,12 +501,14 @@ def tile_sinkhornrouter_kernel(tc, x_bytes, x_scale, w_gate, out):
                 out=now["vv"][:, 1, :], in0=now["v"][:], in1=now["vv"][:, 0, :], op=ALU.subtract
             )
 
+        cols_of = {"n": WIDE}
+
         def rows_open():
             now["u"] = small.tile([P, TILES], F32, name="u%d" % last)
             now["uu"] = small.tile([P, 2, TILES], BF16, name="uu%d" % last)
             now["sums"] = small.tile([P, TILES], F32, name="sums%d" % last)
             for lo, hi in halves:
-                now["rps%d" % lo] = ps_x.tile([P, hi - lo, W_ALL], F32, name="xt")
+                now["rps%d" % lo] = ps_x.tile([P, hi - lo, 2 * cols_of["n"]], F32, name="xt")
 
         def rows(part, j0, j1):
             for j in range(j0, j1):
@@ -509,24 +516,24 @@ def tile_sinkhornrouter_kernel(tc, x_bytes, x_scale, w_gate, out):
                 rps = now["rps%d" % lo]
                 if part == 1:
                     nc.tensor.matmul(
-                        out=rps[:, j - lo, 0:W_LO], lhsT=two_t[last][:, j, 1, :],
-                        rhs=now["vv"][:, 0, :].to_broadcast([P, W_LO]), start=True, stop=True,
+                        out=rps[:, j - lo, 0 : cols_of["n"]], lhsT=two_t[last][:, j, 1, :],
+                        rhs=now["vv"][:, 0, :].to_broadcast([P, cols_of["n"]]), start=True, stop=True,
                     )
                 else:
                     nc.tensor.matmul(
-                        out=rps[:, j - lo, W_LO:W_ALL].rearrange("p (r t) -> p r t", t=2),
+                        out=rps[:, j - lo, cols_of["n"] : 2 * cols_of["n"]].rearrange("p (r t) -> p r t", t=2),
                         lhsT=two_t[last][:, j, 0, :],
-                        rhs=now["vv"][:].rearrange("p t o -> p o t").to_broadcast([P, REP, 2]),
+                        rhs=now["vv"][:].rearrange("p t o -> p o t").to_broadcast([P, cols_of["n"] // 2, 2]),
                         start=True, stop=True,
                     )
 
         def u_first(lo, hi):
             with low_precision():
-                nc.vector.reciprocal(out=now["uu"][:, 0, lo:hi], in_=now["rps%d" % lo][:, :, W_LO])
+                nc.vector.reciprocal(out=now["uu"][:, 0, lo:hi], in_=now["rps%d" % lo][:, :, cols_of["n"]])
 
         def u_sum(lo, hi):
             nc.vector.tensor_reduce(
-                out=now["sums"][:, lo:hi], in_=now["rps%d" % lo][:, :, W_LO - 1 : W_LO + 2], axis=AX.X, op=ALU.add
+                out=now["sums"][:, lo:hi], in_=now["rps%d" % lo][:, :, cols_of["n"] - 1 : cols_of["n"] + 2], axis=AX.X, op=ALU.add
             )
 
         def u_full(lo, hi):
@@ -542,15 +549,15 @@ def tile_sinkhornrouter_kernel(tc, x_bytes, x_scale, w_gate, out):
             for j in range(j0, j1):
                 if part == 1:
                     nc.tensor.matmul(
-                        out=cps[:, 0:W_LO], lhsT=two_b[last][:, j, 1, :],
-                        rhs=now["uu"][:, 0, j : j + 1].to_broadcast([P, W_LO]),
+                        out=cps[:, 0 : cols_of["n"]], lhsT=two_b[last][:, j, 1, :],
+                        rhs=now["uu"][:, 0, j : j + 1].to_broadcast([P, cols_of["n"]]),
                         start=(j == 0), stop=(j == TILES - 1),
                     )
                 else:
                     nc.tensor.matmul(
-                        out=cps[:, W_LO:W_ALL].rearrange("p (r t) -> p r t", t=2),
+                        out=cps[:, cols_of["n"] : 2 * cols_of["n"]].rearrange("p (r t) -> p r t", t=2),
                         lhsT=two_b[last][:, j, 0, :],
-                        rhs=now["uu"][:, :, j : j + 1].rearrange("p t o -> p o t").to_broadcast([P, REP, 2]),
+                        rhs=now["uu"][:, :, j : j + 1].rearrange("p t o -> p o t").to_broadcast([P, cols_of["n"] // 2, 2]),
                         start=(j == 0), stop=(j == TILES - 1),
                     )
 
@@ -560,6 +567,7 @@ def tile_sinkhornrouter_kernel(tc, x_bytes, x_scale, w_gate, out):
         v_first(now["total"][:])
         for rnd in range(ROUNDS):
             final = rnd == ROUNDS - 1
+            cols_of["n"] = WIDE if rnd < WIDE_ROUNDS else NARROW
             rows_open()
             if rnd == 0:
                 rows(1, 0, TILES - 1)
@@ -594,7 +602,7 @@ def tile_sinkhornrouter_kernel(tc, x_bytes, x_scale, w_gate, out):
                     scale_rows(0, 2 * rnd - 1, False)
                 elif rnd > 2:
                     warm(FILL_U)
-                now["cps"] = ps_x.tile([P, W_ALL], F32, name="xt")
+                now["cps"] = ps_x.tile([P, 2 * cols_of["n"]], F32, name="xt")
                 u_sum(a0, a1)
                 u_first(a0, a1)
                 cols(1, a0, a1)
@@ -616,5 +624,5 @@ def tile_sinkhornrouter_kernel(tc, x_bytes, x_scale, w_gate, out):
                 else:
                     warm(FILL_V)
                 v_open()
-                v_sum(now["cps"][:, W_LO - 1 : W_LO + 2])
-                v_first(now["cps"][:, W_LO : W_LO + 1])
+                v_sum(now["cps"][:, cols_of["n"] - 1 : cols_of["n"] + 2])
+                v_first(now["cps"][:, cols_of["n"] : cols_of["n"] + 1])

@@ -238,9 +238,27 @@ def tile_sinkhornrouter_kernel(tc, x_bytes, x_scale, w_gate, out):
             inverse(den, den if near is None else near, v, vv, 0, 1)
             now["v"] = v
             now["vv"] = vv
+            now["v_terms"] = vv[:]
 
         def rest_v(b):
             rest(state[b]["v"], state[b]["vv"], 0, 1)
+
+        def halves_of(words):
+            n = words[:].shape[2]
+            return words[:].bitcast(BF16)[:, :, 1 : 2 * n : 2]
+
+        def cut_v(source):
+            now = state[0]
+            total = small.tile([P, 1], F32, name="total0")
+            nc.vector.tensor_reduce(out=total[:], in_=source, axis=AX.X, op=ALU.add)
+            words = small.tile([P, 2, 1], F32, name="v_words")
+            nc.vector.reciprocal(out=words[:, 0, :], in_=total[:])
+            now["v_words"] = words
+            now["v_terms"] = halves_of(words).rearrange("p t o -> p o t")
+
+        def cut_rest(words):
+            upper = halves_of(words)
+            nc.vector.tensor_tensor(out=upper[:, 1, :], in0=words[:, 0, :], in1=upper[:, 0, :], op=ALU.subtract)
 
         def col_open(b, rep):
             state[b]["cps"] = bank(b, [P, rep, 2] if rep > 0 else [P, 1])
@@ -252,7 +270,7 @@ def tile_sinkhornrouter_kernel(tc, x_bytes, x_scale, w_gate, out):
                     for part in range(2):
                         nc.tensor.matmul(
                             out=now["cps"][:], lhsT=two_b[b][:, j, part, :],
-                            rhs=now["uu"][:, j : j + 1, :].to_broadcast([P, rep, 2]),
+                            rhs=now["u_terms"](j).to_broadcast([P, rep, 2]),
                             start=(j == 0 and part == 0), stop=(j == TILES - 1 and part == 1),
                         )
                     if b == 0 and j in WARM_AT and len(quiet) == 0:
@@ -273,6 +291,7 @@ def tile_sinkhornrouter_kernel(tc, x_bytes, x_scale, w_gate, out):
             now["u"] = small.tile([P, TILES], F32, name="u%d" % b)
             now["uu"] = small.tile([P, TILES, 2], BF16, name="uu%d" % b)
             now["sums"] = small.tile([P, TILES], F32, name="sums%d" % b)
+            now["u_words"] = small.tile([P, 2, TILES], F32, name="u_words%d" % b)
 
         def row_sums(b, lo, hi, rep):
             now = state[b]
@@ -282,7 +301,7 @@ def tile_sinkhornrouter_kernel(tc, x_bytes, x_scale, w_gate, out):
                     for part in range(2):
                         nc.tensor.matmul(
                             out=rps[:, j - lo, :, :], lhsT=two_t[b][:, j, part, :],
-                            rhs=now["vv"][:].to_broadcast([P, rep, 2]),
+                            rhs=now["v_terms"].to_broadcast([P, rep, 2]),
                             start=(part == 0), stop=(part == 1),
                         )
                     if b == 0 and j in WARM_AT and len(quiet) == 0:
@@ -358,19 +377,30 @@ def tile_sinkhornrouter_kernel(tc, x_bytes, x_scale, w_gate, out):
             nc.sync.dma_start(out=out_view[b][:, js, :], in_=res[b][:, js, :])
 
         def early_v_first():
-            new_v(0, acc[0][:], False, None)
+            cut_v(acc[0][:])
 
         def early_v():
+            cut_v(state[0]["cps"][:, 0, :])
+
+        def last_v():
             new_v(0, state[0]["cps"][:, 0, :], False, state[0]["cps"][:, 0, 0:1])
 
         def early_u():
-            new_u(0, 0, TILES, False, False)
+            now = state[0]
+            words = now["u_words"]
+            nc.vector.tensor_reduce(out=now["sums"][:], in_=now["rps0"][:, :, 0, :], axis=AX.X, op=ALU.add)
+            nc.vector.reciprocal(out=words[:, 0, :], in_=now["sums"][:])
+            upper = halves_of(words)
+            now["u_terms"] = lambda j: upper[:, :, j : j + 1].rearrange("p t o -> p o t")
 
         def early_rest_v():
+            cut_rest(state[0]["v_words"])
+
+        def last_rest_v():
             rest_v(0)
 
         def early_rest_u():
-            rest_u(0, 0, TILES)
+            cut_rest(state[0]["u_words"])
 
         def early_rows():
             row_open(0)
@@ -383,7 +413,10 @@ def tile_sinkhornrouter_kernel(tc, x_bytes, x_scale, w_gate, out):
         early = [(early_v_first, early_rest_v, early_rows)]
         for k in range(1, ROUNDS):
             early.append((early_u, early_rest_u, early_cols))
-            early.append((early_v, early_rest_v, early_rows))
+            if k < ROUNDS - 1:
+                early.append((early_v, early_rest_v, early_rows))
+            else:
+                early.append((last_v, last_rest_v, early_rows))
 
         for i in range(FIRST):
             byte_tiles[i] = byte_pool.tile([P, D], U8, name="x_raw_bytes")

@@ -410,13 +410,22 @@ def tile_sinkhornrouter_kernel(tc, x_bytes, x_scale, w_gate, out):
             col_open(0, 1)
             col_sums(0, 0, TILES, 1)
 
+        def wide_rows():
+            row_open(0)
+            row_sums(0, 0, TILES, WIDE // 2)
+
+        def wide_cols():
+            col_open(0, WIDE // 2)
+            col_sums(0, 0, TILES, WIDE // 2)
+
         early = [(early_v_first, early_rest_v, early_rows)]
         for k in range(1, ROUNDS):
-            early.append((early_u, early_rest_u, early_cols))
             if k < ROUNDS - 1:
+                early.append((early_u, early_rest_u, early_cols))
                 early.append((early_v, early_rest_v, early_rows))
             else:
-                early.append((last_v, last_rest_v, early_rows))
+                early.append((early_u, early_rest_u, wide_cols))
+                early.append((last_v, last_rest_v, wide_rows))
 
         for i in range(FIRST):
             byte_tiles[i] = byte_pool.tile([P, D], U8, name="x_raw_bytes")

@@ -19,26 +19,28 @@ ACT = mybir.ActivationFunctionType
 AX = mybir.AxisListType
 
 P = 128
+K_PASS = 512
+BANK_COLS = 1024
 TILES = N // P
 NT = B * TILES
-PASSES = D // 512
+PASSES = D // K_PASS
+BANKS = D // BANK_COLS
+LAST = B - 1
 AHEAD = 4
-FIRST = 2
-THREE = [(0, 0), (1, 0), (0, 1)]
-SPLIT_GROUPS = [(0, 4), (4, 8), (8, 12), (12, 14), (14, 15), (15, 16)]
-WARM_A = 4
-WARM_B = 0
-WARM_C = 0
-WARM_AT = ()
-FILL_V = 2
-FILL_U = 1
-WIDE_ROUNDS = 3
+HEAD_TILES = 2
+HEAD_BLOCKS = [(0, 512), (512, 1024), (1024, 2048), (2048, 3072), (3072, 4096)]
+W_READY = 3
+LAG = 2
+TERM_GROUPS = [(0, 4), (4, 8), (8, 12), (12, 14), (14, 15), (15, 16)]
+IDLE_LOOP = 4
+IDLE_AFTER_COLS = 2
+IDLE_AFTER_ROWS = 1
 WIDE = 32
 NARROW = 12
-HEAD_COLS = 1024
+WIDE_ROUNDS = 3
+HEAD_COLS = BANK_COLS
 OWN_TWO = (21, 25)
 LAST_PIECES = [(0, 4), (4, 6), (6, 8)]
-OWN_SKIP = 8
 
 
 def tile_sinkhornrouter_kernel(tc, x_bytes, x_scale, w_gate, out):
@@ -50,105 +52,106 @@ def tile_sinkhornrouter_kernel(tc, x_bytes, x_scale, w_gate, out):
     with ExitStack() as ctx:
         const = ctx.enter_context(tc.tile_pool(name="const", bufs=1))
         byte_pool = ctx.enter_context(tc.tile_pool(name="bytes", bufs=AHEAD))
-        wide_pool = ctx.enter_context(tc.tile_pool(name="wide", bufs=3))
-        grp_pool = ctx.enter_context(tc.tile_pool(name="grp", bufs=4))
+        wide_pool = ctx.enter_context(tc.tile_pool(name="wide", bufs=LAG + 1))
+        grp_pool = ctx.enter_context(tc.tile_pool(name="grp", bufs=LAG + 2))
         code_pool = ctx.enter_context(tc.tile_pool(name="code", bufs=3))
         small = ctx.enter_context(tc.tile_pool(name="small", bufs=4))
-        ps_x = ctx.enter_context(tc.psum_pool(name="psx", bufs=4))
-        ps_1 = ctx.enter_context(tc.psum_pool(name="ps1", bufs=1))
+        ps_turn = ctx.enter_context(tc.psum_pool(name="turn", bufs=BANKS))
+        ps_role = ctx.enter_context(tc.psum_pool(name="role", bufs=1))
         ctx.enter_context(tc.manual_schedule())
 
         ident = const.tile([P, P], F32, name="ident")
         make_identity(nc, ident[:])
         ident_bf = const.tile([P, P], BF16, name="ident_bf")
         make_identity(nc, ident_bf[:])
-        sc = const.tile([P, D], F32, name="sc")
-        sc_own = const.tile([P, 2, 4], F32, name="sc_own")
+        scales_all = const.tile([P, D], F32, name="scales_all")
+        scales_own = const.tile([P, 2, 4], F32, name="scales_own")
         w_raw = const.tile([P, D], BF16, name="w_raw")
         w_grp = const.tile([P, D], BF16, name="w_grp", align_bytes=64)
         w_codes = const.tile([P, PASSES * P], U32, name="w_codes", align_bytes=64)
         w_scl = const.tile([P, PASSES * P], U8, name="w_scl", align_bytes=64)
-        p_t = [const.tile([P, TILES, P], F32, name="p_t%d" % b) for b in range(B)]
-        two_t = [const.tile([P, TILES, 2, P], BF16, name="two_t%d" % b) for b in range(B)]
-        two_b = [const.tile([P, TILES, 2, P], BF16, name="two_b%d" % b) for b in range(B)]
+        p_less = [const.tile([P, TILES, P], F32, name="p_less%d" % b) for b in range(B)]
+        terms_e = [const.tile([P, TILES, 2, P], BF16, name="terms_e%d" % b) for b in range(B)]
+        terms_n = [const.tile([P, TILES, 2, P], BF16, name="terms_n%d" % b) for b in range(B)]
         p_v = [const.tile([P, TILES, P], F32, name="p_v%d" % b) for b in range(B)]
         res = [const.tile([P, TILES, P], F32, name="res%d" % b) for b in range(B)]
-        acc = [const.tile([P, TILES + 1], F32, name="acc%d" % b) for b in range(B)]
+        col_sum = [const.tile([P, TILES + 1], F32, name="col_sum%d" % b) for b in range(B)]
         for b in range(B):
-            nc.gpsimd.memset(acc[b][:, TILES : TILES + 1], N * EPS)
-        idle = ps_1.tile([P, 512], F32, name="idle")
+            nc.gpsimd.memset(col_sum[b][:, TILES : TILES + 1], N * EPS)
+        idle_bank = ps_role.tile([P, 512], F32, name="idle")
 
         byte_tiles = {}
         wide_tiles = {}
         grp_tiles = {}
         held = {}
+        first = {}
+        second = {}
+
 
         def load(i):
-            xb = byte_pool.tile([P, D], U8, name="x_raw_bytes")
-            nc.sync.dma_start(out=xb[:], in_=x_view[i // TILES, i % TILES])
-            byte_tiles[i] = xb
+            byte_tiles[i] = byte_pool.tile([P, D], U8, name="x_raw_bytes")
+            nc.sync.dma_start(out=byte_tiles[i][:], in_=x_view[i // TILES, i % TILES])
 
         def own(i):
-            if i == NT - 1 or i < FIRST:
+            if i == NT - 1 or i < HEAD_TILES:
                 return 0
             return 2 if i in OWN_TWO else 1
 
         def cast(i):
-            xs = wide_pool.tile([P, D], BF16, name="xs")
+            wide_tiles[i] = wide_pool.tile([P, D], BF16, name="wide")
             if own(i) > 0:
-                first = D - 512 * own(i)
-                nc.scalar.copy(out=xs[:, first:], in_=byte_tiles[i][:, first:].bitcast(FP8))
-            wide_tiles[i] = xs
+                cols = slice(D - K_PASS * own(i), D)
+                nc.scalar.copy(out=wide_tiles[i][:, cols], in_=byte_tiles[i][:, cols].bitcast(FP8))
 
-        def widen(i, first, end):
-            cols = slice(first, min(end, D - 512 * own(i)))
+        def product(i, start, end):
+            cols = slice(start, min(end, D - K_PASS * own(i)))
             nc.vector.tensor_tensor(
-                out=wide_tiles[i][:, cols], in0=byte_tiles[i][:, cols].bitcast(FP8), in1=sc[:, cols],
+                out=wide_tiles[i][:, cols], in0=byte_tiles[i][:, cols].bitcast(FP8), in1=scales_all[:, cols],
                 op=ALU.mult,
             )
 
-        def turn(src, grp, own, q0=0, q1=PASSES // 2):
+        def turn(src, grp, scaled_later, banks):
             words = src[:].bitcast(F32)
             grp_words = grp[:].bitcast(F32)
-            for q in range(q0, q1):
-                xt = ps_x.tile([P, 2, 2, P], F32, name="xt")
+            for q in banks:
+                bank = ps_turn.tile([P, 2, 2, P], F32, name="turn")
                 for gg in range(2):
                     g = 2 * q + gg
                     for u in range(2):
                         nc.tensor.transpose(
-                            out=xt[:, gg, u, :],
+                            out=bank[:, gg, u, :],
                             in_=words[:, 256 * g + u : 256 * (g + 1) : 2],
                             identity=ident[:],
                         )
-                plain = min(2, max(0, PASSES - own - 2 * q))
+                plain = min(2, max(0, PASSES - scaled_later - 2 * q))
                 if plain > 0:
                     nc.scalar.copy(
                         out=grp_words[:, 512 * q : 512 * q + 256 * plain].rearrange(
                             "p (g r u) -> p g r u", g=plain, u=2
                         ),
-                        in_=xt[:, 0:plain, :, :].rearrange("p g u r -> p g r u"),
+                        in_=bank[:, 0:plain, :, :].rearrange("p g u r -> p g r u"),
                     )
                 if plain < 2:
-                    held["xt"] = xt
+                    held["bank"] = bank
 
-        def turn_own(grp, count):
+        def scale_own(grp, count):
             for gg in range(2 - count, 2):
                 g = PASSES - 2 + gg
                 for u in range(2):
-                    pairs = held["xt"][:, gg, u, :].bitcast(BF16)
+                    pairs = held["bank"][:, gg, u, :].bitcast(BF16)
                     for e in range(2):
                         t = 2 * u + e
                         nc.scalar.activation(
-                            out=grp[:, 512 * g + t : 512 * (g + 1) : 4],
+                            out=grp[:, K_PASS * g + t : K_PASS * (g + 1) : 4],
                             in_=pairs[:, e : 2 * P : 2],
                             func=ACT.Copy,
-                            scale=sc_own[:, gg, t : t + 1],
+                            scale=scales_own[:, gg, t : t + 1],
                         )
 
-        def warm(count):
+        def idle_passes(count):
             for k in range(count):
                 nc.tensor.matmul_mx(
-                    out=idle[:],
+                    out=idle_bank[:],
                     lhsT=w_codes[:, 0:P].bitcast(FP8X4),
                     lhsT_scale=w_scl[:, 0:P],
                     rhs=w_codes[:, 0:512].bitcast(FP8X4),
@@ -162,18 +165,19 @@ def tile_sinkhornrouter_kernel(tc, x_bytes, x_scale, w_gate, out):
             codes = code_pool.tile([P, PASSES * P], U32, name="codes", align_bytes=64)
             scl = code_pool.tile([P, PASSES * P], U8, name="scl", align_bytes=64)
             if i >= NT - 2:
-                gps = ps_x.tile([P, P], F32, name="xt")
+                sums = ps_turn.tile([P, P], F32, name="turn")
             else:
-                gps = ps_1.tile([P, P], F32, name="gps")
+                sums = ps_role.tile([P, P], F32, name="gates")
             for g0, g1 in LAST_PIECES if i == NT - 1 else [(0, PASSES)]:
                 part = slice(P * g0, P * g1)
                 nc.vector.quantize_mx(
-                    out=codes[:, part].bitcast(FP8X4), scales=scl[:, part], in_=grp_tiles[i][:, 512 * g0 : 512 * g1]
+                    out=codes[:, part].bitcast(FP8X4), scales=scl[:, part],
+                    in_=grp_tiles[i][:, K_PASS * g0 : K_PASS * g1],
                 )
                 for g in range(g0, g1):
                     cols = slice(P * g, P * (g + 1))
                     nc.tensor.matmul_mx(
-                        out=gps[:],
+                        out=sums[:],
                         lhsT=w_codes[:, cols].bitcast(FP8X4),
                         lhsT_scale=w_scl[:, cols],
                         rhs=codes[:, cols].bitcast(FP8X4),
@@ -182,489 +186,390 @@ def tile_sinkhornrouter_kernel(tc, x_bytes, x_scale, w_gate, out):
                         stop=(g == PASSES - 1),
                     )
             nc.scalar.activation(
-                out=p_t[b][:, j, :], in_=gps[:], func=ACT.Relu, bias=-EPS, scale=1.0,
-                accum_out=acc[b][:, j : j + 1],
+                out=p_less[b][:, j, :], in_=sums[:], func=ACT.Relu, bias=-EPS, scale=1.0,
+                accum_out=col_sum[b][:, j : j + 1],
             )
-            nc.scalar.activation(out=two_t[b][:, j, 0, :], in_=p_t[b][:, j, :], func=ACT.Copy, bias=EPS, scale=1.0)
+            nc.scalar.activation(
+                out=terms_e[b][:, j, 0, :], in_=p_less[b][:, j, :], func=ACT.Copy, bias=EPS, scale=1.0
+            )
 
         def second_term(b, j0, j1):
             nc.vector.scalar_tensor_tensor(
-                out=two_t[b][:, j0:j1, 1, :], in0=p_t[b][:, j0:j1, :], scalar=EPS,
-                in1=two_t[b][:, j0:j1, 0, :], op0=ALU.add, op1=ALU.subtract,
+                out=terms_e[b][:, j0:j1, 1, :], in0=p_less[b][:, j0:j1, :], scalar=EPS,
+                in1=terms_e[b][:, j0:j1, 0, :], op0=ALU.add, op1=ALU.subtract,
             )
 
-        def flip_terms(b, j0, j1, spare=False):
+        def turn_terms(b, j0, j1, rotating=False):
             for a in range(j0, j1, 2):
                 n = min(2, j1 - a)
-                if spare:
-                    flip = ps_x.tile([P, 2, 2, P], BF16, name="xt")
+                if rotating:
+                    bank = ps_turn.tile([P, 2, 2, P], BF16, name="turn")
                 else:
-                    flip = ps_1.tile([P, 2, 2, P], BF16, name="flip")
+                    bank = ps_role.tile([P, 2, 2, P], BF16, name="terms")
                 for jj in range(n):
-                    for part in range(2):
+                    for term in range(2):
                         nc.tensor.transpose(
-                            out=flip[:, jj, part, :], in_=two_t[b][:, a + jj, part, :],
-                            identity=ident_bf[:],
+                            out=bank[:, jj, term, :], in_=terms_e[b][:, a + jj, term, :], identity=ident_bf[:]
                         )
-                nc.scalar.copy(out=two_b[b][:, a : a + n, :, :], in_=flip[:, 0:n, :, :])
+                nc.scalar.copy(out=terms_n[b][:, a : a + n, :, :], in_=bank[:, 0:n, :, :])
 
-        def inverse(den, near, full, pair, lo, hi):
-            if pair is not None:
-                with nc.allow_low_precision(reason="the first of two bfloat16 terms; the second holds what it drops"):
-                    nc.vector.reciprocal(out=pair[:, lo:hi, 0], in_=near)
-            nc.vector.reciprocal(out=full[:, lo:hi], in_=den)
 
-        def rest(full, pair, lo, hi):
-            nc.vector.tensor_tensor(
-                out=pair[:, lo:hi, 1], in0=full[:, lo:hi], in1=pair[:, lo:hi, 0], op=ALU.subtract
-            )
-
-        state = [{}, {}]
-
-        def bank(b, shape):
-            if b == B - 1:
-                return ps_x.tile(shape, F32, name="xt")
-            return ps_1.tile(shape, F32, name="chain")
-
-        def new_v(b, source, summed, near):
-            now = state[b]
-            den = source
-            if not summed:
-                total = small.tile([P, 1], F32, name="total%d" % b)
-                nc.vector.tensor_reduce(out=total[:], in_=source, axis=AX.X, op=ALU.add)
-                den = total[:]
-            v = small.tile([P, 1], F32, name="v%d" % b)
-            vv = small.tile([P, 1, 2], BF16, name="vv%d" % b)
-            inverse(den, den if near is None else near, v, vv, 0, 1)
-            now["v"] = v
-            now["vv"] = vv
-            now["v_terms"] = vv[:]
-
-        def rest_v(b):
-            rest(state[b]["v"], state[b]["vv"], 0, 1)
-
-        def halves_of(words):
-            n = words[:].shape[2]
-            return words[:].bitcast(BF16)[:, :, 1 : 2 * n : 2]
-
-        def cut_v(source):
-            now = state[0]
-            total = small.tile([P, 1], F32, name="total0")
-            nc.vector.tensor_reduce(out=total[:], in_=source, axis=AX.X, op=ALU.add)
-            words = small.tile([P, 2, 1], F32, name="v_words")
-            nc.vector.reciprocal(out=words[:, 0, :], in_=total[:])
-            now["v_words"] = words
-            now["v_terms"] = halves_of(words).rearrange("p t o -> p o t")
-
-        def cut_rest(words):
-            upper = halves_of(words)
-            nc.vector.tensor_tensor(out=upper[:, 1, :], in0=words[:, 0, :], in1=upper[:, 0, :], op=ALU.subtract)
-
-        def col_open(b, rep):
-            state[b]["cps"] = bank(b, [P, rep, 2] if rep > 0 else [P, 1])
-
-        def col_sums(b, lo, hi, rep):
-            now = state[b]
-            for j in range(lo, hi):
-                if rep > 0:
-                    for part in range(2):
-                        nc.tensor.matmul(
-                            out=now["cps"][:], lhsT=two_b[b][:, j, part, :],
-                            rhs=now["u_terms"](j).to_broadcast([P, rep, 2]),
-                            start=(j == 0 and part == 0), stop=(j == TILES - 1 and part == 1),
-                        )
-                    if b == 0 and j in WARM_AT and len(quiet) == 0:
-                        warm(1)
-                else:
-                    for n in range(3):
-                        part, term = THREE[n]
-                        nc.tensor.matmul(
-                            out=now["cps"][:], lhsT=two_b[b][:, j, part, :],
-                            rhs=now["uu"][:, j, term : term + 1],
-                            start=(j == 0 and n == 0), stop=(j == TILES - 1 and n == 2),
-                        )
-                    if j in WARM_AT:
-                        warm(1)
-
-        def row_open(b):
-            now = state[b]
-            now["u"] = small.tile([P, TILES], F32, name="u%d" % b)
-            now["uu"] = small.tile([P, TILES, 2], BF16, name="uu%d" % b)
-            now["sums"] = small.tile([P, TILES], F32, name="sums%d" % b)
-            now["u_words"] = small.tile([P, 2, TILES], F32, name="u_words%d" % b)
-
-        def row_sums(b, lo, hi, rep):
-            now = state[b]
-            rps = bank(b, [P, hi - lo, rep, 2] if rep > 0 else [P, hi - lo])
-            for j in range(lo, hi):
-                if rep > 0:
-                    for part in range(2):
-                        nc.tensor.matmul(
-                            out=rps[:, j - lo, :, :], lhsT=two_t[b][:, j, part, :],
-                            rhs=now["v_terms"].to_broadcast([P, rep, 2]),
-                            start=(part == 0), stop=(part == 1),
-                        )
-                    if b == 0 and j in WARM_AT and len(quiet) == 0:
-                        warm(1)
-                else:
-                    for n in range(3):
-                        part, term = THREE[n]
-                        nc.tensor.matmul(
-                            out=rps[:, j - lo : j - lo + 1], lhsT=two_t[b][:, j, part, :],
-                            rhs=now["vv"][:, 0, term : term + 1],
-                            start=(n == 0), stop=(n == 2),
-                        )
-                    if j in WARM_AT:
-                        warm(1)
-            now["rps%d" % lo] = rps
-
-        def new_u(b, lo, hi, final, summed):
-            now = state[b]
-            den = now["rps%d" % lo][:]
-            near = den
-            if not summed:
-                nc.vector.tensor_reduce(
-                    out=now["sums"][:, lo:hi], in_=now["rps%d" % lo][:, :, 0, :], axis=AX.X, op=ALU.add
-                )
-                den = now["sums"][:, lo:hi]
-                near = now["rps%d" % lo][:, :, 0, 0]
-            inverse(den, near, now["u"], None if final else now["uu"], lo, hi)
-
-        def rest_u(b, lo, hi):
-            rest(state[b]["u"], state[b]["uu"], lo, hi)
-
-        def scale_columns(b, q, on_vector):
-            v = state[b]["v"]
+        def times_v(b, v, q, on_vector):
             js = slice(4 * q, 4 * q + 4)
             if on_vector:
                 nc.vector.tensor_scalar(
-                    out=p_v[b][:, js, :], in0=p_t[b][:, js, :], scalar1=EPS, scalar2=v[:, 0:1],
+                    out=p_v[b][:, js, :], in0=p_less[b][:, js, :], scalar1=EPS, scalar2=v[:, 0:1],
                     op0=ALU.add, op1=ALU.mult,
                 )
             else:
-                if "ev" not in state[b]:
-                    ev = small.tile([P, 1], F32, name="ev%d" % b)
-                    nc.scalar.activation(out=ev[:], in_=v[:], func=ACT.Copy, scale=EPS)
-                    state[b]["ev"] = ev
+                if ("eps_v", b) not in held:
+                    held[("eps_v", b)] = small.tile([P, 1], F32, name="eps_v%d" % b)
+                    nc.scalar.activation(out=held[("eps_v", b)][:], in_=v[:], func=ACT.Copy, scale=EPS)
                 nc.scalar.activation(
-                    out=p_v[b][:, js, :], in_=p_t[b][:, js, :], func=ACT.Identity,
-                    scale=v[:, 0:1], bias=state[b]["ev"][:, 0:1],
+                    out=p_v[b][:, js, :], in_=p_less[b][:, js, :], func=ACT.Identity,
+                    scale=v[:, 0:1], bias=held[("eps_v", b)][:, 0:1],
                 )
 
         def turn_back(b, q):
-            back = ps_x.tile([P, 4, P], F32, name="xt")
+            bank = ps_turn.tile([P, 4, P], F32, name="turn")
             for jj in range(4):
-                nc.tensor.transpose(
-                    out=back[:, jj, :], in_=p_v[b][:, 4 * q + jj, :], identity=ident[:]
-                )
-            state[b]["back%d" % q] = back
+                nc.tensor.transpose(out=bank[:, jj, :], in_=p_v[b][:, 4 * q + jj, :], identity=ident[:])
+            held[("back", b, q)] = bank
 
-        def scale_rows(b, q, on_vector):
-            u = state[b]["u"]
-            back = state[b]["back%d" % q]
+        def times_u(b, u, q, on_vector):
+            bank = held[("back", b, q)]
             js = slice(4 * q, 4 * q + 4)
             if on_vector:
                 nc.vector.tensor_tensor(
-                    out=res[b][:, js, :], in0=back[:],
+                    out=res[b][:, js, :], in0=bank[:],
                     in1=u[:, js].unsqueeze(2).to_broadcast([P, 4, P]), op=ALU.mult,
                 )
             else:
                 for jj in range(4):
                     j = 4 * q + jj
                     nc.scalar.activation(
-                        out=res[b][:, j, :], in_=back[:, jj, :], func=ACT.Copy, scale=u[:, j : j + 1]
+                        out=res[b][:, j, :], in_=bank[:, jj, :], func=ACT.Copy, scale=u[:, j : j + 1]
                     )
             nc.sync.dma_start(out=out_view[b][:, js, :], in_=res[b][:, js, :])
-
-        def early_v_first():
-            cut_v(acc[0][:])
-
-        def early_v():
-            cut_v(state[0]["cps"][:, 0, :])
-
-        def last_v():
-            new_v(0, state[0]["cps"][:, 0, :], False, state[0]["cps"][:, 0, 0:1])
-
-        def early_u():
-            now = state[0]
-            words = now["u_words"]
-            nc.vector.tensor_reduce(out=now["sums"][:], in_=now["rps0"][:, :, 0, :], axis=AX.X, op=ALU.add)
-            nc.vector.reciprocal(out=words[:, 0, :], in_=now["sums"][:])
-            upper = halves_of(words)
-            now["u_terms"] = lambda j: upper[:, :, j : j + 1].rearrange("p t o -> p o t")
-
-        def early_rest_v():
-            cut_rest(state[0]["v_words"])
-
-        def last_rest_v():
-            rest_v(0)
-
-        def early_rest_u():
-            cut_rest(state[0]["u_words"])
-
-        def early_rows():
-            row_open(0)
-            row_sums(0, 0, TILES, 1)
-
-        def early_cols():
-            col_open(0, 1)
-            col_sums(0, 0, TILES, 1)
-
-        def wide_rows():
-            row_open(0)
-            row_sums(0, 0, TILES, WIDE // 2)
-
-        def wide_cols():
-            col_open(0, WIDE // 2)
-            col_sums(0, 0, TILES, WIDE // 2)
-
-        early = [(early_v_first, early_rest_v, early_rows)]
-        for k in range(1, ROUNDS):
-            if k < ROUNDS - 1:
-                early.append((early_u, early_rest_u, early_cols))
-                early.append((early_v, early_rest_v, early_rows))
-            else:
-                early.append((early_u, early_rest_u, wide_cols))
-                early.append((last_v, last_rest_v, wide_rows))
-
-        for i in range(FIRST):
-            byte_tiles[i] = byte_pool.tile([P, D], U8, name="x_raw_bytes")
-            wide_tiles[i] = wide_pool.tile([P, D], BF16, name="xs")
-            grp_tiles[i] = grp_pool.tile([P, D], BF16, name="grp", align_bytes=64)
-        for c in range(4):
-            cols = slice(1024 * c, 1024 * (c + 1))
-            nc.sync.dma_start(out=sc[:, cols], in_=scale_row[cols].partition_broadcast(P))
-            for i in range(FIRST):
-                nc.sync.dma_start(out=byte_tiles[i][:, cols], in_=x_view[0, i][:, cols])
-        nc.sync.dma_start(
-            out=sc_own[:],
-            in_=x_scale.rearrange("a b (g p t) -> p (a b g) t", p=P, t=4)[:, PASSES - 2 :, :],
-        )
-        load(FIRST)
-        nc.sync.dma_start(out=w_raw[:], in_=w_gate)
-        for i in range(FIRST + 1, AHEAD):
-            load(i)
-        for c in range(4):
-            for i in range(FIRST):
-                widen(i, 1024 * c, 1024 * (c + 1))
-                turn(wide_tiles[i], grp_tiles[i], 0, c, c + 1)
-
-        EARLY_FROM = TILES + 2
-        LAST_EARLY = NT
-        done = 0
-        pending = []
-        quiet = []
-        late = []
-        for i in range(NT + 2):
-            if i < FIRST:
-                at = 0
-            elif i < NT and len(pending) > 0:
-                widen(i, 0, HEAD_COLS)
-            elif i < NT:
-                widen(i, 0, D)
-            for entry in pending:
-                entry[1]()
-                entry[2]()
-                warm(WARM_B)
-            ahead = 0 < i < NT - 1 and len(pending) > 0
-            if ahead:
-                gates(i - 2)
-                warm(WARM_C)
-            if i == NT - 1:
-                for first in range(HEAD_COLS, D, 1024):
-                    widen(i, first, first + 1024)
-            elif 0 < i < NT and len(pending) > 0:
-                widen(i, HEAD_COLS, D)
-            pending.clear()
-            if i < NT:
-                if i + AHEAD < NT:
-                    load(i + AHEAD)
-            if FIRST <= i < NT:
-                grp_tiles[i] = grp_pool.tile([P, D], BF16, name="grp", align_bytes=64)
-                turn(wide_tiles[i], grp_tiles[i], own(i))
-            if i == 0:
-                turn(w_raw, w_grp, 0)
-            if i == 2:
-                nc.vector.quantize_mx(out=w_codes[:].bitcast(FP8X4), scales=w_scl[:], in_=w_grp[:])
-            k = i - 3
-            if k >= 0:
-                for j0, j1 in SPLIT_GROUPS:
-                    if k % TILES == j1 - 1 and i < NT:
-                        second_term(k // TILES, j0, j1)
-                        flip_terms(k // TILES, j0, j1)
-                    elif k % TILES == j1 - 1:
-                        late.append((k // TILES, j0, j1))
-            if i >= 2 and not ahead:
-                gates(i - 2)
-            if 2 <= i < NT and own(i) > 0:
-                turn_own(grp_tiles[i], own(i))
-            if FIRST <= i + 1 < NT:
-                cast(i + 1)
-            if EARLY_FROM <= i < LAST_EARLY and done < len(early):
-                early[done][0]()
-                pending.append(early[done])
-                done += 1
-            elif 2 <= i < NT:
-                warm(WARM_A)
-
-        last = B - 1
-        halves = [(0, TILES // 2), (TILES // 2, TILES)]
-        now = state[last]
-        left = early[done:]
-        left[0][0]()
-        left[0][1]()
-        quiet.append(1)
-        left[0][2]()
-        assert len(left) == 1
-        for entry in late:
-            second_term(entry[0], entry[1], entry[2])
-            flip_terms(entry[0], entry[1], entry[2], entry[1] == TILES - 2)
 
         def low_precision():
             return nc.allow_low_precision(reason="the first of two bfloat16 terms; the second holds what it drops")
 
+
+        def upper_halves(words):
+            n = words[:].shape[2]
+            return words[:].bitcast(BF16)[:, :, 1 : 2 * n : 2]
+
+        def cut_second_term(words):
+            upper = upper_halves(words)
+            nc.vector.tensor_tensor(out=upper[:, 1, :], in0=words[:, 0, :], in1=upper[:, 0, :], op=ALU.subtract)
+
+        def first_v(source):
+            total = small.tile([P, 1], F32, name="total0")
+            nc.vector.tensor_reduce(out=total[:], in_=source, axis=AX.X, op=ALU.add)
+            first["v_words"] = small.tile([P, 2, 1], F32, name="v_words")
+            nc.vector.reciprocal(out=first["v_words"][:, 0, :], in_=total[:])
+            first["v_terms"] = upper_halves(first["v_words"]).rearrange("p t o -> p o t")
+
+        def first_v_from_tiles():
+            first_v(col_sum[0][:])
+
+        def first_v_from_sums():
+            first_v(first["cols"][:, 0, :])
+
+        def first_v_second():
+            cut_second_term(first["v_words"])
+
+        def first_v_last():
+            total = small.tile([P, 1], F32, name="total0")
+            nc.vector.tensor_reduce(out=total[:], in_=first["cols"][:, 0, :], axis=AX.X, op=ALU.add)
+            first["v"] = small.tile([P, 1], F32, name="v0")
+            first["vv"] = small.tile([P, 1, 2], BF16, name="vv0")
+            with low_precision():
+                nc.vector.reciprocal(out=first["vv"][:, 0:1, 0], in_=first["cols"][:, 0, 0:1])
+            nc.vector.reciprocal(out=first["v"][:, 0:1], in_=total[:])
+            first["v_terms"] = first["vv"][:]
+
+        def first_v_last_second():
+            nc.vector.tensor_tensor(
+                out=first["vv"][:, 0:1, 1], in0=first["v"][:, 0:1], in1=first["vv"][:, 0:1, 0], op=ALU.subtract
+            )
+
+        def first_u():
+            nc.vector.tensor_reduce(out=first["sums"][:], in_=first["rows"][:, :, 0, :], axis=AX.X, op=ALU.add)
+            nc.vector.reciprocal(out=first["u_words"][:, 0, :], in_=first["sums"][:])
+
+        def first_u_second():
+            cut_second_term(first["u_words"])
+
+        def first_rows(copies):
+            first["sums"] = small.tile([P, TILES], F32, name="sums0")
+            first["u_words"] = small.tile([P, 2, TILES], F32, name="u_words0")
+            first["rows"] = ps_role.tile([P, TILES, copies, 2], F32, name="chain")
+            for j in range(TILES):
+                for term in range(2):
+                    nc.tensor.matmul(
+                        out=first["rows"][:, j, :, :], lhsT=terms_e[0][:, j, term, :],
+                        rhs=first["v_terms"].to_broadcast([P, copies, 2]),
+                        start=(term == 0), stop=(term == 1),
+                    )
+
+        def first_cols(copies):
+            first["cols"] = ps_role.tile([P, copies, 2], F32, name="chain")
+            upper = upper_halves(first["u_words"])
+            for j in range(TILES):
+                for term in range(2):
+                    nc.tensor.matmul(
+                        out=first["cols"][:], lhsT=terms_n[0][:, j, term, :],
+                        rhs=upper[:, :, j : j + 1].rearrange("p t o -> p o t").to_broadcast([P, copies, 2]),
+                        start=(j == 0 and term == 0), stop=(j == TILES - 1 and term == 1),
+                    )
+
+        def first_rows_once():
+            first_rows(1)
+
+        def first_cols_once():
+            first_cols(1)
+
+        def first_rows_wide():
+            first_rows(WIDE // 2)
+
+        def first_cols_wide():
+            first_cols(WIDE // 2)
+
+        steps = [(first_v_from_tiles, first_v_second, first_rows_once)]
+        for rnd in range(1, ROUNDS - 1):
+            steps.append((first_u, first_u_second, first_cols_once))
+            steps.append((first_v_from_sums, first_v_second, first_rows_once))
+        steps.append((first_u, first_u_second, first_cols_wide))
+        steps.append((first_v_last, first_v_last_second, first_rows_wide))
+
+        for i in range(HEAD_TILES):
+            byte_tiles[i] = byte_pool.tile([P, D], U8, name="x_raw_bytes")
+            wide_tiles[i] = wide_pool.tile([P, D], BF16, name="wide")
+            grp_tiles[i] = grp_pool.tile([P, D], BF16, name="grp", align_bytes=64)
+        for start, end in HEAD_BLOCKS:
+            cols = slice(start, end)
+            nc.sync.dma_start(out=scales_all[:, cols], in_=scale_row[cols].partition_broadcast(P))
+            for i in range(HEAD_TILES):
+                nc.sync.dma_start(out=byte_tiles[i][:, cols], in_=x_view[0, i][:, cols])
+        nc.sync.dma_start(
+            out=scales_own[:],
+            in_=x_scale.rearrange("a b (g p t) -> p (a b g) t", p=P, t=4)[:, PASSES - 2 :, :],
+        )
+        load(HEAD_TILES)
+        nc.sync.dma_start(out=w_raw[:], in_=w_gate)
+        for i in range(HEAD_TILES + 1, AHEAD):
+            load(i)
+        for start, end in HEAD_BLOCKS:
+            for i in range(HEAD_TILES):
+                product(i, start, end)
+                if end % BANK_COLS == 0:
+                    turn(wide_tiles[i], grp_tiles[i], 0, [end // BANK_COLS - 1])
+
+        first_step = TILES + LAG
+        step = None
+        steps_done = 0
+        late = []
+        for i in range(NT + LAG):
+            beside_chain = step is not None
+            if HEAD_TILES <= i < NT:
+                product(i, 0, HEAD_COLS if beside_chain else D)
+            if beside_chain:
+                step[1]()
+                step[2]()
+            inside = beside_chain and i < NT - 1
+            if inside:
+                gates(i - LAG)
+            if i == NT - 1:
+                for q in range(1, BANKS):
+                    product(i, BANK_COLS * q, BANK_COLS * (q + 1))
+            elif beside_chain and i < NT:
+                product(i, HEAD_COLS, D)
+            step = None
+            if i + AHEAD < NT:
+                load(i + AHEAD)
+            if HEAD_TILES <= i < NT:
+                grp_tiles[i] = grp_pool.tile([P, D], BF16, name="grp", align_bytes=64)
+                turn(wide_tiles[i], grp_tiles[i], own(i), range(BANKS))
+            if i == 0:
+                turn(w_raw, w_grp, 0, range(BANKS))
+            if i == W_READY:
+                nc.vector.quantize_mx(out=w_codes[:].bitcast(FP8X4), scales=w_scl[:], in_=w_grp[:])
+                gates(0)
+            clamped = i - LAG - 1
+            for j0, j1 in TERM_GROUPS:
+                if clamped >= 0 and clamped % TILES == j1 - 1:
+                    if i < NT:
+                        second_term(clamped // TILES, j0, j1)
+                        turn_terms(clamped // TILES, j0, j1)
+                    else:
+                        late.append((j0, j1))
+            if i >= W_READY and not inside:
+                gates(i - LAG)
+            if LAG <= i < NT and own(i) > 0:
+                scale_own(grp_tiles[i], own(i))
+            if HEAD_TILES <= i + 1 < NT:
+                cast(i + 1)
+            if first_step <= i < NT:
+                step = steps[steps_done]
+                steps_done += 1
+                step[0]()
+            elif W_READY <= i < NT:
+                idle_passes(IDLE_LOOP)
+
+        assert steps_done == len(steps) - 1
+        for part in steps[steps_done]:
+            part()
+        for j0, j1 in late:
+            second_term(LAST, j0, j1)
+            turn_terms(LAST, j0, j1, j0 == TILES - 2)
+
+        halves = [(0, TILES // 2), (TILES // 2, TILES)]
+        (a0, a1), (b0, b1) = halves
+
         def v_open():
-            now["v"] = small.tile([P, 1], F32, name="v%d" % last)
-            now["vv"] = small.tile([P, 2, 1], BF16, name="vv%d" % last)
-            now["total"] = small.tile([P, 1], F32, name="total%d" % last)
+            second["v"] = small.tile([P, 1], F32, name="v%d" % LAST)
+            second["vv"] = small.tile([P, 2, 1], BF16, name="vv%d" % LAST)
+            second["total"] = small.tile([P, 1], F32, name="total%d" % LAST)
 
         def v_first(near):
             with low_precision():
-                nc.vector.reciprocal(out=now["vv"][:, 0, :], in_=near)
+                nc.vector.reciprocal(out=second["vv"][:, 0, :], in_=near)
 
         def v_sum(source):
-            nc.vector.tensor_reduce(out=now["total"][:], in_=source, axis=AX.X, op=ALU.add)
+            nc.vector.tensor_reduce(out=second["total"][:], in_=source, axis=AX.X, op=ALU.add)
 
         def v_full():
-            nc.vector.reciprocal(out=now["v"][:], in_=now["total"][:])
+            nc.vector.reciprocal(out=second["v"][:], in_=second["total"][:])
 
         def v_second():
             nc.vector.tensor_tensor(
-                out=now["vv"][:, 1, :], in0=now["v"][:], in1=now["vv"][:, 0, :], op=ALU.subtract
+                out=second["vv"][:, 1, :], in0=second["v"][:], in1=second["vv"][:, 0, :], op=ALU.subtract
             )
 
-        cols_of = {"n": WIDE}
-
-        def rows_open():
-            now["u"] = small.tile([P, TILES], F32, name="u%d" % last)
-            now["uu"] = small.tile([P, 2, TILES], BF16, name="uu%d" % last)
-            now["sums"] = small.tile([P, TILES], F32, name="sums%d" % last)
+        def rows_open(width):
+            second["u"] = small.tile([P, TILES], F32, name="u%d" % LAST)
+            second["uu"] = small.tile([P, 2, TILES], BF16, name="uu%d" % LAST)
+            second["sums"] = small.tile([P, TILES], F32, name="sums%d" % LAST)
             for lo, hi in halves:
-                now["rps%d" % lo] = ps_x.tile([P, hi - lo, 2 * cols_of["n"]], F32, name="xt")
+                second[("rows", lo)] = ps_turn.tile([P, hi - lo, 2 * width], F32, name="turn")
 
-        def rows(part, j0, j1):
+        def rows(term, j0, j1, width):
             for j in range(j0, j1):
-                lo = [a for a, b in halves if a <= j < b][0]
-                rps = now["rps%d" % lo]
-                if part == 1:
+                lo = a0 if j < a1 else b0
+                sums = second[("rows", lo)]
+                if term == 1:
                     nc.tensor.matmul(
-                        out=rps[:, j - lo, 0 : cols_of["n"]], lhsT=two_t[last][:, j, 1, :],
-                        rhs=now["vv"][:, 0, :].to_broadcast([P, cols_of["n"]]), start=True, stop=True,
+                        out=sums[:, j - lo, 0:width], lhsT=terms_e[LAST][:, j, 1, :],
+                        rhs=second["vv"][:, 0, :].to_broadcast([P, width]), start=True, stop=True,
                     )
                 else:
                     nc.tensor.matmul(
-                        out=rps[:, j - lo, cols_of["n"] : 2 * cols_of["n"]].rearrange("p (r t) -> p r t", t=2),
-                        lhsT=two_t[last][:, j, 0, :],
-                        rhs=now["vv"][:].rearrange("p t o -> p o t").to_broadcast([P, cols_of["n"] // 2, 2]),
+                        out=sums[:, j - lo, width : 2 * width].rearrange("p (r t) -> p r t", t=2),
+                        lhsT=terms_e[LAST][:, j, 0, :],
+                        rhs=second["vv"][:].rearrange("p t o -> p o t").to_broadcast([P, width // 2, 2]),
                         start=True, stop=True,
                     )
 
-        def u_first(lo, hi):
+        def u_first(lo, hi, width):
             with low_precision():
-                nc.vector.reciprocal(out=now["uu"][:, 0, lo:hi], in_=now["rps%d" % lo][:, :, cols_of["n"]])
+                nc.vector.reciprocal(out=second["uu"][:, 0, lo:hi], in_=second[("rows", lo)][:, :, width])
 
-        def u_sum(lo, hi):
+        def u_sum(lo, hi, width):
             nc.vector.tensor_reduce(
-                out=now["sums"][:, lo:hi], in_=now["rps%d" % lo][:, :, cols_of["n"] - 1 : cols_of["n"] + 2], axis=AX.X, op=ALU.add
+                out=second["sums"][:, lo:hi], in_=second[("rows", lo)][:, :, width - 1 : width + 2],
+                axis=AX.X, op=ALU.add,
             )
 
         def u_full(lo, hi):
-            nc.vector.reciprocal(out=now["u"][:, lo:hi], in_=now["sums"][:, lo:hi])
+            nc.vector.reciprocal(out=second["u"][:, lo:hi], in_=second["sums"][:, lo:hi])
 
         def u_second(lo, hi):
             nc.vector.tensor_tensor(
-                out=now["uu"][:, 1, lo:hi], in0=now["u"][:, lo:hi], in1=now["uu"][:, 0, lo:hi], op=ALU.subtract
+                out=second["uu"][:, 1, lo:hi], in0=second["u"][:, lo:hi], in1=second["uu"][:, 0, lo:hi],
+                op=ALU.subtract,
             )
 
-        def cols(part, j0, j1):
-            cps = now["cps"]
+        def cols(term, j0, j1, width):
             for j in range(j0, j1):
-                if part == 1:
+                if term == 1:
                     nc.tensor.matmul(
-                        out=cps[:, 0 : cols_of["n"]], lhsT=two_b[last][:, j, 1, :],
-                        rhs=now["uu"][:, 0, j : j + 1].to_broadcast([P, cols_of["n"]]),
+                        out=second["cols"][:, 0:width], lhsT=terms_n[LAST][:, j, 1, :],
+                        rhs=second["uu"][:, 0, j : j + 1].to_broadcast([P, width]),
                         start=(j == 0), stop=(j == TILES - 1),
                     )
                 else:
                     nc.tensor.matmul(
-                        out=cps[:, cols_of["n"] : 2 * cols_of["n"]].rearrange("p (r t) -> p r t", t=2),
-                        lhsT=two_b[last][:, j, 0, :],
-                        rhs=now["uu"][:, :, j : j + 1].rearrange("p t o -> p o t").to_broadcast([P, cols_of["n"] // 2, 2]),
+                        out=second["cols"][:, width : 2 * width].rearrange("p (r t) -> p r t", t=2),
+                        lhsT=terms_n[LAST][:, j, 0, :],
+                        rhs=second["uu"][:, :, j : j + 1].rearrange("p t o -> p o t").to_broadcast([P, width // 2, 2]),
                         start=(j == 0), stop=(j == TILES - 1),
                     )
 
-        (a0, a1), (b0, b1) = halves
         v_open()
-        v_sum(acc[last][:])
-        v_first(now["total"][:])
+        v_sum(col_sum[LAST][:])
+        v_first(second["total"][:])
         for rnd in range(ROUNDS):
-            final = rnd == ROUNDS - 1
-            cols_of["n"] = WIDE if rnd < WIDE_ROUNDS else NARROW
-            rows_open()
+            width = WIDE if rnd < WIDE_ROUNDS else NARROW
+            rows_open(width)
             if rnd == 0:
-                rows(1, 0, TILES - 1)
-                second_term(last, TILES - 1, TILES)
+                rows(1, 0, TILES - 1, width)
+                second_term(LAST, TILES - 1, TILES)
                 v_full()
                 v_second()
-                rows(1, TILES - 1, TILES)
+                rows(1, TILES - 1, TILES, width)
             else:
-                rows(1, 0, TILES)
+                rows(1, 0, TILES, width)
                 v_full()
                 v_second()
-            rows(0, a0, a1)
-            rows(0, b0, b1)
+            rows(0, a0, a1, width)
+            rows(0, b0, b1, width)
             if rnd == 0:
-                flip_terms(last, TILES - 1, TILES)
+                turn_terms(LAST, TILES - 1, TILES)
                 for q in range(4):
-                    scale_columns(0, q, False)
-            if final:
-                scale_columns(last, 0, True)
-                scale_columns(last, 1, True)
-                scale_columns(last, 2, False)
-                scale_columns(last, 3, False)
+                    times_v(0, first["v"], q, False)
+            if rnd == ROUNDS - 1:
+                times_v(LAST, second["v"], 0, True)
+                times_v(LAST, second["v"], 1, True)
+                times_v(LAST, second["v"], 2, False)
+                times_v(LAST, second["v"], 3, False)
                 for lo, hi in halves:
-                    u_sum(lo, hi)
+                    u_sum(lo, hi, width)
                     u_full(lo, hi)
                 for q in range(4):
-                    turn_back(last, q)
-                    scale_rows(last, q, q % 2 == 0)
+                    turn_back(LAST, q)
+                    times_u(LAST, second["u"], q, q % 2 == 0)
             else:
                 if 1 <= rnd <= 2:
                     turn_back(0, 2 * rnd - 1)
-                    scale_rows(0, 2 * rnd - 1, False)
+                    times_u(0, first["u"], 2 * rnd - 1, False)
                 elif rnd > 2:
-                    warm(FILL_U)
-                now["cps"] = ps_x.tile([P, 2 * cols_of["n"]], F32, name="xt")
-                u_sum(a0, a1)
-                u_first(a0, a1)
-                cols(1, a0, a1)
-                u_sum(b0, b1)
+                    idle_passes(IDLE_AFTER_ROWS)
+                second["cols"] = ps_turn.tile([P, 2 * width], F32, name="turn")
+                u_sum(a0, a1, width)
+                u_first(a0, a1, width)
+                cols(1, a0, a1, width)
+                u_sum(b0, b1, width)
                 u_full(a0, a1)
-                u_first(b0, b1)
-                cols(1, b0, b1)
+                u_first(b0, b1, width)
+                cols(1, b0, b1, width)
                 u_full(b0, b1)
                 u_second(a0, a1)
-                cols(0, a0, a1)
+                cols(0, a0, a1, width)
                 u_second(b0, b1)
-                cols(0, b0, b1)
+                cols(0, b0, b1, width)
                 if rnd == 0:
-                    new_u(0, 0, TILES, True, False)
+                    nc.vector.tensor_reduce(
+                        out=first["sums"][:], in_=first["rows"][:, :, 0, :], axis=AX.X, op=ALU.add
+                    )
+                    first["u"] = small.tile([P, TILES], F32, name="u0")
+                    nc.vector.reciprocal(out=first["u"][:], in_=first["sums"][:])
                 if rnd < 2:
                     turn_back(0, 2 * rnd)
-                    scale_rows(0, 2 * rnd, False)
-                    warm(max(0, FILL_V - 2))
+                    times_u(0, first["u"], 2 * rnd, False)
                 else:
-                    warm(FILL_V)
+                    idle_passes(IDLE_AFTER_COLS)
                 v_open()
-                v_sum(now["cps"][:, cols_of["n"] - 1 : cols_of["n"] + 2])
-                v_first(now["cps"][:, cols_of["n"] : cols_of["n"] + 1])
+                v_sum(second["cols"][:, width - 1 : width + 2])
+                v_first(second["cols"][:, width : width + 1])

@@ -373,18 +373,19 @@ def tile_sinkhornrouter_kernel(tc, x_bytes, x_scale, w_gate, out):
         late = []
         for i in range(NT + LAG):
             beside_chain = step is not None
+            cut = beside_chain or W_READY < i < NT
             if HEAD_TILES <= i < NT:
-                product(i, 0, HEAD_COLS if beside_chain else D)
+                product(i, 0, HEAD_COLS if cut else D)
             if beside_chain:
                 step[1]()
                 step[2]()
-            inside = beside_chain and i < NT - 1
+            inside = cut and i < NT - 1
             if inside:
                 gates(i - LAG)
             if i == NT - 1:
                 for q in range(1, BANKS):
                     product(i, BANK_COLS * q, BANK_COLS * (q + 1))
-            elif beside_chain and i < NT:
+            elif cut and i < NT:
                 product(i, HEAD_COLS, D)
             step = None
             if i + AHEAD < NT:

from contextlib import ExitStack

import concourse.mybir as mybir
from concourse.masks import make_identity

B, N, D, E = 2, 2048, 4096, 128
EPS = 1e-6
ROUNDS = 8
FLOPS = 2 * B * N * D * E

F32 = mybir.dt.float32
BF16 = mybir.dt.bfloat16
U32 = mybir.dt.uint32
U8 = mybir.dt.uint8
FP8 = mybir.dt.float8_e4m3fn
FP8X4 = mybir.dt.float8_e4m3fn_x4
ALU = mybir.AluOpType
ACT = mybir.ActivationFunctionType
AX = mybir.AxisListType

P = 128
K_PASS = 512
BANK_COLS = 1024
TILES = N // P
NT = B * TILES
PASSES = D // K_PASS
BANKS = D // BANK_COLS
LAST = B - 1
AHEAD = 4
HEAD_TILES = 2
HEAD_BLOCKS = [(0, 512), (512, 1024), (1024, 2048), (2048, 3072), (3072, 4096)]
W_READY = 3
LAG = 2
TERM_GROUPS = [(0, 4), (4, 8), (8, 12), (12, 14), (14, 15), (15, 16)]
IDLE_LOOP = 4
IDLE_AFTER_COLS = 2
IDLE_AFTER_ROWS = 1
WIDE = 32
NARROW = 12
WIDE_ROUNDS = 3
HEAD_COLS = BANK_COLS
OWN_TWO = (21, 25)
LAST_PIECES = [(0, 4), (4, 6), (6, 8)]


def tile_sinkhornrouter_kernel(tc, x_bytes, x_scale, w_gate, out):
    nc = tc.nc
    x_view = x_bytes.rearrange("b (p j) k -> b j p k", j=TILES)
    out_view = out.rearrange("b (p j) e -> b p j e", j=TILES)
    scale_row = x_scale.rearrange("a b k -> (a b k)")

    with ExitStack() as ctx:
        const = ctx.enter_context(tc.tile_pool(name="const", bufs=1))
        byte_pool = ctx.enter_context(tc.tile_pool(name="bytes", bufs=AHEAD))
        wide_pool = ctx.enter_context(tc.tile_pool(name="wide", bufs=LAG + 1))
        grp_pool = ctx.enter_context(tc.tile_pool(name="grp", bufs=LAG + 2))
        code_pool = ctx.enter_context(tc.tile_pool(name="code", bufs=3))
        small = ctx.enter_context(tc.tile_pool(name="small", bufs=4))
        ps_turn = ctx.enter_context(tc.psum_pool(name="turn", bufs=BANKS))
        ps_role = ctx.enter_context(tc.psum_pool(name="role", bufs=1))
        ctx.enter_context(tc.manual_schedule())

        ident = const.tile([P, P], F32, name="ident")
        make_identity(nc, ident[:])
        ident_bf = const.tile([P, P], BF16, name="ident_bf")
        make_identity(nc, ident_bf[:])
        scales_all = const.tile([P, D], F32, name="scales_all")
        scales_own = const.tile([P, 2, 4], F32, name="scales_own")
        w_raw = const.tile([P, D], BF16, name="w_raw")
        w_grp = const.tile([P, D], BF16, name="w_grp", align_bytes=64)
        w_codes = const.tile([P, PASSES * P], U32, name="w_codes", align_bytes=64)
        w_scl = const.tile([P, PASSES * P], U8, name="w_scl", align_bytes=64)
        p_less = [const.tile([P, TILES, P], F32, name="p_less%d" % b) for b in range(B)]
        terms_e = [const.tile([P, TILES, 2, P], BF16, name="terms_e%d" % b) for b in range(B)]
        terms_n = [const.tile([P, TILES, 2, P], BF16, name="terms_n%d" % b) for b in range(B)]
        p_v = [const.tile([P, TILES, P], F32, name="p_v%d" % b) for b in range(B)]
        res = [const.tile([P, TILES, P], F32, name="res%d" % b) for b in range(B)]
        col_sum = [const.tile([P, TILES + 1], F32, name="col_sum%d" % b) for b in range(B)]
        for b in range(B):
            nc.gpsimd.memset(col_sum[b][:, TILES : TILES + 1], N * EPS)
        idle_bank = ps_role.tile([P, 512], F32, name="idle")

        byte_tiles = {}
        wide_tiles = {}
        grp_tiles = {}
        held = {}
        first = {}
        second = {}


        def load(i):
            byte_tiles[i] = byte_pool.tile([P, D], U8, name="x_raw_bytes")
            nc.sync.dma_start(out=byte_tiles[i][:], in_=x_view[i // TILES, i % TILES])

        def own(i):
            if i == NT - 1 or i < HEAD_TILES:
                return 0
            return 2 if i in OWN_TWO else 1

        def cast(i):
            wide_tiles[i] = wide_pool.tile([P, D], BF16, name="wide")
            if own(i) > 0:
                cols = slice(D - K_PASS * own(i), D)
                nc.scalar.copy(out=wide_tiles[i][:, cols], in_=byte_tiles[i][:, cols].bitcast(FP8))

        def product(i, start, end):
            cols = slice(start, min(end, D - K_PASS * own(i)))
            nc.vector.tensor_tensor(
                out=wide_tiles[i][:, cols], in0=byte_tiles[i][:, cols].bitcast(FP8), in1=scales_all[:, cols],
                op=ALU.mult,
            )

        def turn(src, grp, scaled_later, banks):
            words = src[:].bitcast(F32)
            grp_words = grp[:].bitcast(F32)
            for q in banks:
                bank = ps_turn.tile([P, 2, 2, P], F32, name="turn")
                for gg in range(2):
                    g = 2 * q + gg
                    for u in range(2):
                        nc.tensor.transpose(
                            out=bank[:, gg, u, :],
                            in_=words[:, 256 * g + u : 256 * (g + 1) : 2],
                            identity=ident[:],
                        )
                plain = min(2, max(0, PASSES - scaled_later - 2 * q))
                if plain > 0:
                    nc.scalar.copy(
                        out=grp_words[:, 512 * q : 512 * q + 256 * plain].rearrange(
                            "p (g r u) -> p g r u", g=plain, u=2
                        ),
                        in_=bank[:, 0:plain, :, :].rearrange("p g u r -> p g r u"),
                    )
                if plain < 2:
                    held["bank"] = bank

        def scale_own(grp, count):
            for gg in range(2 - count, 2):
                g = PASSES - 2 + gg
                for u in range(2):
                    pairs = held["bank"][:, gg, u, :].bitcast(BF16)
                    for e in range(2):
                        t = 2 * u + e
                        nc.scalar.activation(
                            out=grp[:, K_PASS * g + t : K_PASS * (g + 1) : 4],
                            in_=pairs[:, e : 2 * P : 2],
                            func=ACT.Copy,
                            scale=scales_own[:, gg, t : t + 1],
                        )

        def idle_passes(count):
            for k in range(count):
                nc.tensor.matmul_mx(
                    out=idle_bank[:],
                    lhsT=w_codes[:, 0:P].bitcast(FP8X4),
                    lhsT_scale=w_scl[:, 0:P],
                    rhs=w_codes[:, 0:512].bitcast(FP8X4),
                    rhs_scale=w_scl[:, 0:512],
                    start=True,
                    stop=True,
                )

        def gates(i):
            b, j = i // TILES, i % TILES
            codes = code_pool.tile([P, PASSES * P], U32, name="codes", align_bytes=64)
            scl = code_pool.tile([P, PASSES * P], U8, name="scl", align_bytes=64)
            if i >= NT - 2:
                sums = ps_turn.tile([P, P], F32, name="turn")
            else:
                sums = ps_role.tile([P, P], F32, name="gates")
            for g0, g1 in LAST_PIECES if i == NT - 1 else [(0, PASSES)]:
                part = slice(P * g0, P * g1)
                nc.vector.quantize_mx(
                    out=codes[:, part].bitcast(FP8X4), scales=scl[:, part],
                    in_=grp_tiles[i][:, K_PASS * g0 : K_PASS * g1],
                )
                for g in range(g0, g1):
                    cols = slice(P * g, P * (g + 1))
                    nc.tensor.matmul_mx(
                        out=sums[:],
                        lhsT=w_codes[:, cols].bitcast(FP8X4),
                        lhsT_scale=w_scl[:, cols],
                        rhs=codes[:, cols].bitcast(FP8X4),
                        rhs_scale=scl[:, cols],
                        start=(g == 0),
                        stop=(g == PASSES - 1),
                    )
            nc.scalar.activation(
                out=p_less[b][:, j, :], in_=sums[:], func=ACT.Relu, bias=-EPS, scale=1.0,
                accum_out=col_sum[b][:, j : j + 1],
            )
            nc.scalar.activation(
                out=terms_e[b][:, j, 0, :], in_=p_less[b][:, j, :], func=ACT.Copy, bias=EPS, scale=1.0
            )

        def second_term(b, j0, j1):
            nc.vector.scalar_tensor_tensor(
                out=terms_e[b][:, j0:j1, 1, :], in0=p_less[b][:, j0:j1, :], scalar=EPS,
                in1=terms_e[b][:, j0:j1, 0, :], op0=ALU.add, op1=ALU.subtract,
            )

        def turn_terms(b, j0, j1, rotating=False):
            for a in range(j0, j1, 2):
                n = min(2, j1 - a)
                if rotating:
                    bank = ps_turn.tile([P, 2, 2, P], BF16, name="turn")
                else:
                    bank = ps_role.tile([P, 2, 2, P], BF16, name="terms")
                for jj in range(n):
                    for term in range(2):
                        nc.tensor.transpose(
                            out=bank[:, jj, term, :], in_=terms_e[b][:, a + jj, term, :], identity=ident_bf[:]
                        )
                nc.scalar.copy(out=terms_n[b][:, a : a + n, :, :], in_=bank[:, 0:n, :, :])


        def times_v(b, v, q, on_vector):
            js = slice(4 * q, 4 * q + 4)
            if on_vector:
                nc.vector.tensor_scalar(
                    out=p_v[b][:, js, :], in0=p_less[b][:, js, :], scalar1=EPS, scalar2=v[:, 0:1],
                    op0=ALU.add, op1=ALU.mult,
                )
            else:
                if ("eps_v", b) not in held:
                    held[("eps_v", b)] = small.tile([P, 1], F32, name="eps_v%d" % b)
                    nc.scalar.activation(out=held[("eps_v", b)][:], in_=v[:], func=ACT.Copy, scale=EPS)
                nc.scalar.activation(
                    out=p_v[b][:, js, :], in_=p_less[b][:, js, :], func=ACT.Identity,
                    scale=v[:, 0:1], bias=held[("eps_v", b)][:, 0:1],
                )

        def turn_back(b, q):
            bank = ps_turn.tile([P, 4, P], F32, name="turn")
            for jj in range(4):
                nc.tensor.transpose(out=bank[:, jj, :], in_=p_v[b][:, 4 * q + jj, :], identity=ident[:])
            held[("back", b, q)] = bank

        def times_u(b, u, q, on_vector):
            bank = held[("back", b, q)]
            js = slice(4 * q, 4 * q + 4)
            if on_vector:
                nc.vector.tensor_tensor(
                    out=res[b][:, js, :], in0=bank[:],
                    in1=u[:, js].unsqueeze(2).to_broadcast([P, 4, P]), op=ALU.mult,
                )
            else:
                for jj in range(4):
                    j = 4 * q + jj
                    nc.scalar.activation(
                        out=res[b][:, j, :], in_=bank[:, jj, :], func=ACT.Copy, scale=u[:, j : j + 1]
                    )
            nc.sync.dma_start(out=out_view[b][:, js, :], in_=res[b][:, js, :])

        def low_precision():
            return nc.allow_low_precision(reason="the first of two bfloat16 terms; the second holds what it drops")


        def upper_halves(words):
            n = words[:].shape[2]
            return words[:].bitcast(BF16)[:, :, 1 : 2 * n : 2]

        def cut_second_term(words):
            upper = upper_halves(words)
            nc.vector.tensor_tensor(out=upper[:, 1, :], in0=words[:, 0, :], in1=upper[:, 0, :], op=ALU.subtract)

        def first_v(source):
            total = small.tile([P, 1], F32, name="total0")
            nc.vector.tensor_reduce(out=total[:], in_=source, axis=AX.X, op=ALU.add)
            first["v_words"] = small.tile([P, 2, 1], F32, name="v_words")
            nc.vector.reciprocal(out=first["v_words"][:, 0, :], in_=total[:])
            first["v_terms"] = upper_halves(first["v_words"]).rearrange("p t o -> p o t")

        def first_v_from_tiles():
            first_v(col_sum[0][:])

        def first_v_from_sums():
            first_v(first["cols"][:, 0, :])

        def first_v_second():
            cut_second_term(first["v_words"])

        def first_v_last():
            total = small.tile([P, 1], F32, name="total0")
            nc.vector.tensor_reduce(out=total[:], in_=first["cols"][:, 0, :], axis=AX.X, op=ALU.add)
            first["v"] = small.tile([P, 1], F32, name="v0")
            first["vv"] = small.tile([P, 1, 2], BF16, name="vv0")
            with low_precision():
                nc.vector.reciprocal(out=first["vv"][:, 0:1, 0], in_=first["cols"][:, 0, 0:1])
            nc.vector.reciprocal(out=first["v"][:, 0:1], in_=total[:])
            first["v_terms"] = first["vv"][:]

        def first_v_last_second():
            nc.vector.tensor_tensor(
                out=first["vv"][:, 0:1, 1], in0=first["v"][:, 0:1], in1=first["vv"][:, 0:1, 0], op=ALU.subtract
            )

        def first_u():
            nc.vector.tensor_reduce(out=first["sums"][:], in_=first["rows"][:, :, 0, :], axis=AX.X, op=ALU.add)
            nc.vector.reciprocal(out=first["u_words"][:, 0, :], in_=first["sums"][:])

        def first_u_second():
            cut_second_term(first["u_words"])

        def first_rows(copies):
            first["sums"] = small.tile([P, TILES], F32, name="sums0")
            first["u_words"] = small.tile([P, 2, TILES], F32, name="u_words0")
            first["rows"] = ps_role.tile([P, TILES, copies, 2], F32, name="chain")
            for j in range(TILES):
                for term in range(2):
                    nc.tensor.matmul(
                        out=first["rows"][:, j, :, :], lhsT=terms_e[0][:, j, term, :],
                        rhs=first["v_terms"].to_broadcast([P, copies, 2]),
                        start=(term == 0), stop=(term == 1),
                    )

        def first_cols(copies):
            first["cols"] = ps_role.tile([P, copies, 2], F32, name="chain")
            upper = upper_halves(first["u_words"])
            for j in range(TILES):
                for term in range(2):
                    nc.tensor.matmul(
                        out=first["cols"][:], lhsT=terms_n[0][:, j, term, :],
                        rhs=upper[:, :, j : j + 1].rearrange("p t o -> p o t").to_broadcast([P, copies, 2]),
                        start=(j == 0 and term == 0), stop=(j == TILES - 1 and term == 1),
                    )

        def first_rows_once():
            first_rows(1)

        def first_cols_once():
            first_cols(1)

        def first_rows_wide():
            first_rows(WIDE // 2)

        def first_cols_wide():
            first_cols(WIDE // 2)

        steps = [(first_v_from_tiles, first_v_second, first_rows_once)]
        for rnd in range(1, ROUNDS - 1):
            steps.append((first_u, first_u_second, first_cols_once))
            steps.append((first_v_from_sums, first_v_second, first_rows_once))
        steps.append((first_u, first_u_second, first_cols_wide))
        steps.append((first_v_last, first_v_last_second, first_rows_wide))

        for i in range(HEAD_TILES):
            byte_tiles[i] = byte_pool.tile([P, D], U8, name="x_raw_bytes")
            wide_tiles[i] = wide_pool.tile([P, D], BF16, name="wide")
            grp_tiles[i] = grp_pool.tile([P, D], BF16, name="grp", align_bytes=64)
        for start, end in HEAD_BLOCKS:
            cols = slice(start, end)
            nc.sync.dma_start(out=scales_all[:, cols], in_=scale_row[cols].partition_broadcast(P))
            for i in range(HEAD_TILES):
                nc.sync.dma_start(out=byte_tiles[i][:, cols], in_=x_view[0, i][:, cols])
        nc.sync.dma_start(
            out=scales_own[:],
            in_=x_scale.rearrange("a b (g p t) -> p (a b g) t", p=P, t=4)[:, PASSES - 2 :, :],
        )
        load(HEAD_TILES)
        nc.sync.dma_start(out=w_raw[:], in_=w_gate)
        for i in range(HEAD_TILES + 1, AHEAD):
            load(i)
        for start, end in HEAD_BLOCKS:
            for i in range(HEAD_TILES):
                product(i, start, end)
                if end % BANK_COLS == 0:
                    turn(wide_tiles[i], grp_tiles[i], 0, [end // BANK_COLS - 1])

        first_step = TILES + LAG
        step = None
        steps_done = 0
        late = []
        for i in range(NT + LAG):
            beside_chain = step is not None
            cut = beside_chain or W_READY < i < NT
            if HEAD_TILES <= i < NT:
                product(i, 0, HEAD_COLS if cut else D)
            if beside_chain:
                step[1]()
                step[2]()
            inside = cut and i < NT - 1
            if inside:
                gates(i - LAG)
            if i == NT - 1:
                for q in range(1, BANKS):
                    product(i, BANK_COLS * q, BANK_COLS * (q + 1))
            elif cut and i < NT:
                product(i, HEAD_COLS, D)
            step = None
            if i + AHEAD < NT:
                load(i + AHEAD)
            if HEAD_TILES <= i < NT:
                grp_tiles[i] = grp_pool.tile([P, D], BF16, name="grp", align_bytes=64)
                turn(wide_tiles[i], grp_tiles[i], own(i), range(BANKS))
            if i == 0:
                turn(w_raw, w_grp, 0, range(BANKS))
            if i == W_READY:
                nc.vector.quantize_mx(out=w_codes[:].bitcast(FP8X4), scales=w_scl[:], in_=w_grp[:])
                gates(0)
            clamped = i - LAG - 1
            for j0, j1 in TERM_GROUPS:
                if clamped >= 0 and clamped % TILES == j1 - 1:
                    if i < NT:
                        second_term(clamped // TILES, j0, j1)
                        turn_terms(clamped // TILES, j0, j1)
                    else:
                        late.append((j0, j1))
            if i >= W_READY and not inside:
                gates(i - LAG)
            if LAG <= i < NT and own(i) > 0:
                scale_own(grp_tiles[i], own(i))
            if HEAD_TILES <= i + 1 < NT:
                cast(i + 1)
            if first_step <= i < NT:
                step = steps[steps_done]
                steps_done += 1
                step[0]()
            elif W_READY <= i < NT:
                idle_passes(IDLE_LOOP)

        assert steps_done == len(steps) - 1
        for part in steps[steps_done]:
            part()
        for j0, j1 in late:
            second_term(LAST, j0, j1)
            turn_terms(LAST, j0, j1, j0 == TILES - 2)

        halves = [(0, TILES // 2), (TILES // 2, TILES)]
        (a0, a1), (b0, b1) = halves

        def v_open():
            second["v"] = small.tile([P, 1], F32, name="v%d" % LAST)
            second["vv"] = small.tile([P, 2, 1], BF16, name="vv%d" % LAST)
            second["total"] = small.tile([P, 1], F32, name="total%d" % LAST)

        def v_first(near):
            with low_precision():
                nc.vector.reciprocal(out=second["vv"][:, 0, :], in_=near)

        def v_sum(source):
            nc.vector.tensor_reduce(out=second["total"][:], in_=source, axis=AX.X, op=ALU.add)

        def v_full():
            nc.vector.reciprocal(out=second["v"][:], in_=second["total"][:])

        def v_second():
            nc.vector.tensor_tensor(
                out=second["vv"][:, 1, :], in0=second["v"][:], in1=second["vv"][:, 0, :], op=ALU.subtract
            )

        def rows_open(width):
            second["u"] = small.tile([P, TILES], F32, name="u%d" % LAST)
            second["uu"] = small.tile([P, 2, TILES], BF16, name="uu%d" % LAST)
            second["sums"] = small.tile([P, TILES], F32, name="sums%d" % LAST)
            for lo, hi in halves:
                second[("rows", lo)] = ps_turn.tile([P, hi - lo, 2 * width], F32, name="turn")

        def rows(term, j0, j1, width):
            for j in range(j0, j1):
                lo = a0 if j < a1 else b0
                sums = second[("rows", lo)]
                if term == 1:
                    nc.tensor.matmul(
                        out=sums[:, j - lo, 0:width], lhsT=terms_e[LAST][:, j, 1, :],
                        rhs=second["vv"][:, 0, :].to_broadcast([P, width]), start=True, stop=True,
                    )
                else:
                    nc.tensor.matmul(
                        out=sums[:, j - lo, width : 2 * width].rearrange("p (r t) -> p r t", t=2),
                        lhsT=terms_e[LAST][:, j, 0, :],
                        rhs=second["vv"][:].rearrange("p t o -> p o t").to_broadcast([P, width // 2, 2]),
                        start=True, stop=True,
                    )

        def u_first(lo, hi, width):
            with low_precision():
                nc.vector.reciprocal(out=second["uu"][:, 0, lo:hi], in_=second[("rows", lo)][:, :, width])

        def u_sum(lo, hi, width):
            nc.vector.tensor_reduce(
                out=second["sums"][:, lo:hi], in_=second[("rows", lo)][:, :, width - 1 : width + 2],
                axis=AX.X, op=ALU.add,
            )

        def u_full(lo, hi):
            nc.vector.reciprocal(out=second["u"][:, lo:hi], in_=second["sums"][:, lo:hi])

        def u_second(lo, hi):
            nc.vector.tensor_tensor(
                out=second["uu"][:, 1, lo:hi], in0=second["u"][:, lo:hi], in1=second["uu"][:, 0, lo:hi],
                op=ALU.subtract,
            )

        def cols(term, j0, j1, width):
            for j in range(j0, j1):
                if term == 1:
                    nc.tensor.matmul(
                        out=second["cols"][:, 0:width], lhsT=terms_n[LAST][:, j, 1, :],
                        rhs=second["uu"][:, 0, j : j + 1].to_broadcast([P, width]),
                        start=(j == 0), stop=(j == TILES - 1),
                    )
                else:
                    nc.tensor.matmul(
                        out=second["cols"][:, width : 2 * width].rearrange("p (r t) -> p r t", t=2),
                        lhsT=terms_n[LAST][:, j, 0, :],
                        rhs=second["uu"][:, :, j : j + 1].rearrange("p t o -> p o t").to_broadcast([P, width // 2, 2]),
                        start=(j == 0), stop=(j == TILES - 1),
                    )

        v_open()
        v_sum(col_sum[LAST][:])
        v_first(second["total"][:])
        for rnd in range(ROUNDS):
            width = WIDE if rnd < WIDE_ROUNDS else NARROW
            rows_open(width)
            if rnd == 0:
                rows(1, 0, TILES - 1, width)
                second_term(LAST, TILES - 1, TILES)
                v_full()
                v_second()
                rows(1, TILES - 1, TILES, width)
            else:
                rows(1, 0, TILES, width)
                v_full()
                v_second()
            rows(0, a0, a1, width)
            rows(0, b0, b1, width)
            if rnd == 0:
                turn_terms(LAST, TILES - 1, TILES)
                for q in range(4):
                    times_v(0, first["v"], q, False)
            if rnd == ROUNDS - 1:
                times_v(LAST, second["v"], 0, True)
                times_v(LAST, second["v"], 1, True)
                times_v(LAST, second["v"], 2, False)
                times_v(LAST, second["v"], 3, False)
                for lo, hi in halves:
                    u_sum(lo, hi, width)
                    u_full(lo, hi)
                for q in range(4):
                    turn_back(LAST, q)
                    times_u(LAST, second["u"], q, q % 2 == 0)
            else:
                if 1 <= rnd <= 2:
                    turn_back(0, 2 * rnd - 1)
                    times_u(0, first["u"], 2 * rnd - 1, False)
                elif rnd > 2:
                    idle_passes(IDLE_AFTER_ROWS)
                second["cols"] = ps_turn.tile([P, 2 * width], F32, name="turn")
                u_sum(a0, a1, width)
                u_first(a0, a1, width)
                cols(1, a0, a1, width)
                u_sum(b0, b1, width)
                u_full(a0, a1)
                u_first(b0, b1, width)
                cols(1, b0, b1, width)
                u_full(b0, b1)
                u_second(a0, a1)
                cols(0, a0, a1, width)
                u_second(b0, b1)
                cols(0, b0, b1, width)
                if rnd == 0:
                    nc.vector.tensor_reduce(
                        out=first["sums"][:], in_=first["rows"][:, :, 0, :], axis=AX.X, op=ALU.add
                    )
                    first["u"] = small.tile([P, TILES], F32, name="u0")
                    nc.vector.reciprocal(out=first["u"][:], in_=first["sums"][:])
                if rnd < 2:
                    turn_back(0, 2 * rnd)
                    times_u(0, first["u"], 2 * rnd, False)
                else:
                    idle_passes(IDLE_AFTER_COLS)
                v_open()
                v_sum(second["cols"][:, width - 1 : width + 2])
                v_first(second["cols"][:, width : width + 1])
